import numpy as np
import ml_dtypes


def mxq(x, axis, fmt="e4m3"):
    dtype, down = {"e4m3": (ml_dtypes.float8_e4m3fn, 7), "e5m2": (ml_dtypes.float8_e5m2, 14)}[fmt]
    v = np.moveaxis(np.asarray(x, np.float32).astype(ml_dtypes.bfloat16).astype(np.float64), axis, -1)
    blocks = v.reshape(v.shape[:-1] + (-1, 32))
    amax = np.abs(blocks).max(-1, keepdims=True)
    byte = np.maximum(np.where(amax > 0, np.frexp(amax)[1] - 1 + 127, 0) - down, 1)
    scale = np.exp2(byte - 127.0)
    codes = (blocks / scale).astype(np.float32).astype(dtype).astype(np.float64)
    return np.moveaxis((codes * scale).reshape(v.shape), -1, axis)


WIDE = False


def mx_kscale(k):
    if not WIDE:
        return np.ones(k)
    levels = np.array([10, -10, 5, -5, 0])
    a = np.random.permutation(np.resize(levels, k // 512 * 4)).reshape(k // 512, 4)
    idx = np.arange(k)
    return np.exp2(a[idx // 512, idx % 128 // 32])


BF16 = ml_dtypes.bfloat16


def bf(x):
    return np.asarray(x, np.float32).astype(BF16)


def f64(x):
    return np.asarray(x).astype(np.float64)


E2M1 = np.array([0.0, 0.5, 1.0, 1.5, 2.0, 3.0, 4.0, 6.0, -0.0, -0.5, -1.0, -1.5, -2.0, -3.0, -4.0, -6.0])


def pack_weight(w, fmt):
    k, n = w.shape
    w = f64(bf(w)).reshape(k // 32, 32, n)
    amax = np.abs(w).max(1)
    if fmt == "e4m3":
        byte = np.frexp(amax)[1] - 1 + 127 - 7
    else:
        mant, ex = np.frexp(amax / 6.0)
        byte = np.where(mant > 0.5, ex, ex - 1) + 127
    byte = np.clip(np.where(amax > 0, byte, 1), 1, 254)
    scaled = (w * np.exp2(127.0 - byte)[:, None, :]).reshape(k, n).astype(np.float32)
    by_word = np.ascontiguousarray(scaled.reshape(k // 512, 128, 4, n).transpose(0, 1, 3, 2))
    if fmt == "e4m3":
        words = by_word.astype(ml_dtypes.float8_e4m3fn).view(np.uint8)
    else:
        c = by_word.astype(ml_dtypes.float4_e2m1fn).view(np.uint8) & 0xF
        words = c[..., 0::2] | (c[..., 1::2] << 4)
    return np.ascontiguousarray(words), np.ascontiguousarray(byte.astype(np.uint8).reshape(k // 512, 16, n))


def unpack_weight(words, scales, fmt):
    g, p, n, _ = words.shape
    if fmt == "e4m3":
        vals = np.ascontiguousarray(words).view(ml_dtypes.float8_e4m3fn).astype(np.float64)
    else:
        nib = np.empty((g, p, n, 4), np.uint8)
        nib[..., 0::2] = words & 0xF
        nib[..., 1::2] = words >> 4
        vals = E2M1[nib]
    vals = vals * np.repeat(np.exp2(scales.astype(np.float64) - 127.0), 8, axis=1)[..., None]
    return vals.transpose(0, 1, 3, 2).reshape(g * 512, n)

def pack4(w):
    words, scales = pack_weight(w, "e2m1")
    return words.reshape(words.shape[0], 128, -1), scales


def unpack4(words, scales):
    return unpack_weight(words.reshape(words.shape[0], 128, -1, 2), scales, "e2m1")


B, D_IN, H1, H2, H3, C = 8192, 2048, 2048, 2048, 1024, 512
BN_EPS = 1e-5


def bn_relu(z, gamma, beta):
    m = z.mean(axis=0)
    v = z.var(axis=0)
    return np.maximum((z - m) * (1.0 / np.sqrt(v + BN_EPS)) * gamma + beta, 0.0)


def setup_inputs():
    t = mx_kscale(H3)
    c = 32.0 * np.exp2(-15.0 * np.random.random(H3))
    mu = 0.5 * np.random.standard_normal(H3)
    z2 = bf((np.random.standard_normal((B, H3)) + mu) * c)
    g2 = bf((1.0 + 0.1 * np.random.standard_normal(H3)) * t)
    beta2 = bf(0.2 * np.random.standard_normal(H3) * t)
    w3 = np.random.standard_normal((C, H3)) * 3.0 / np.sqrt(H3) / t
    words, scales = pack4(np.ascontiguousarray(w3.T))
    b3 = bf(0.5 * np.random.standard_normal(C))
    return {"z2": z2,
            "g2": g2,
            "beta2": beta2,
            "W3_words": words,
            "W3_scales": scales,
            "b3": b3}


def reference(z2, g2, beta2, W3_words, W3_scales, b3):
    h = bn_relu(f64(z2), f64(g2), f64(beta2))
    logits = (mxq(h, 1, "e4m3") @ unpack4(W3_words, W3_scales)) + f64(b3)
    s = logits - logits.max(axis=1, keepdims=True)
    return s - np.log(np.exp(s).sum(axis=1, keepdims=True))

@@ -1,0 +1,272 @@
+from contextlib import ExitStack
+
+import concourse.mybir as mybir
+from concourse.masks import make_identity
+
+F32 = mybir.dt.float32
+BF16 = mybir.dt.bfloat16
+I32 = mybir.dt.int32
+U8 = mybir.dt.uint8
+U32 = mybir.dt.uint32
+FP8X4 = mybir.dt.float8_e4m3fn_x4
+FP4X4 = mybir.dt.float4_e2m1fn_x4
+ALU = mybir.AluOpType
+ACT = mybir.ActivationFunctionType
+AXIS = mybir.AxisListType
+
+P = 128
+ROWS, FEATURES, CLASSES = 8192, 1024, 512
+BN_EPS = 1e-5
+PASSES = FEATURES // (4 * P)
+UNITS = 2 * PASSES
+COLS = 4 * PASSES
+TILES = ROWS // P
+GROUP_TILES = 4
+GROUPS = TILES // GROUP_TILES
+GROUP_ROWS = GROUP_TILES * P
+LN_GROUPS = 4
+STAT_RUN = 512
+STAT_CHUNKS = 2 * ROWS // STAT_RUN
+SCALAR_UNIT = 0
+
+FLOPS = 2 * ROWS * FEATURES * CLASSES
+
+
+def transpose_words(nc, zt_pool, ident, z_group, unit):
+    g, u = divmod(unit, 2)
+    zt = zt_pool.tile([P, GROUP_TILES, P], F32)
+    for j in range(GROUP_TILES):
+        nc.tensor.transpose(zt[:, j, :], z_group[:, j, 256 * g + u : 256 * (g + 1) : 2], ident[:])
+    return zt
+
+
+def as_values(zt):
+    return zt[:].rearrange("p j r -> p (j r)").bitcast(BF16)
+
+
+def as_pairs(zt):
+    return as_values(zt).rearrange("p (r e) -> p r e", e=2)
+
+
+def tile_binarymlp_pb_t_kernel(tc, z2, g2, beta2, W3_words, W3_scales, b3, out):
+    nc = tc.nc
+    z_rows = z2.rearrange("(p j) k -> p j k", j=TILES)
+    out_rows = out.rearrange("(p j) n -> p j n", j=TILES)
+
+    with ExitStack() as ctx:
+        const = ctx.enter_context(tc.tile_pool(name="const", bufs=1))
+        resident = ctx.enter_context(tc.tile_pool(name="resident", bufs=1))
+        work = ctx.enter_context(tc.tile_pool(name="work", bufs=2))
+        scratch = ctx.enter_context(tc.tile_pool(name="scratch", bufs=4))
+        zt_pool = ctx.enter_context(tc.psum_pool(name="zt_pool", bufs=UNITS))
+        acc_pool = ctx.enter_context(tc.psum_pool(name="acc_pool", bufs=GROUP_TILES))
+        ctx.enter_context(tc.manual_schedule())
+
+        z_groups = []
+        for c in range(GROUPS):
+            z_group = resident.tile([P, GROUP_TILES, CLASSES], F32, name="z_group%d" % c)
+            nc.sync.dma_start(
+                out=z_group[:].bitcast(BF16),
+                in_=z_rows[:, GROUP_TILES * c : GROUP_TILES * (c + 1), :],
+            )
+            z_groups.append(z_group)
+
+        w_scales = const.tile([P, PASSES, CLASSES], U8, align_bytes=64)
+        nc.vector.memset(w_scales[:].bitcast(I32), 0)
+        w_words = const.tile([P, PASSES, 2 * CLASSES], U8, align_bytes=64)
+        for g in range(PASSES):
+            nc.sync.dma_start(out=w_words[:, g, :].bitcast(I32), in_=W3_words[g].bitcast(I32))
+        for q in range(4):
+            nc.sync.dma_start(
+                out=w_scales[32 * q : 32 * q + 4, :, :].bitcast(I32),
+                in_=W3_scales.bitcast(I32)[:, 4 * q : 4 * q + 4, :].rearrange("g r n -> r g n"),
+            )
+
+        gain_bf = const.tile([P, PASSES, 4], BF16)
+        beta_bf = const.tile([P, PASSES, 4], BF16)
+        bias_bf = const.tile([P, CLASSES], BF16)
+        with nc.allow_non_contiguous_dma(reason="four neighbouring features to a partition"):
+            nc.scalar.dma_start(out=gain_bf[:], in_=g2.rearrange("(g p t) -> p g t", g=PASSES, t=4))
+            nc.scalar.dma_start(out=beta_bf[:], in_=beta2.rearrange("(g p t) -> p g t", g=PASSES, t=4))
+        nc.scalar.dma_start(out=bias_bf[:], in_=b3.partition_broadcast(P))
+        neg_half = const.tile([P, COLS], F32)
+        nc.vector.memset(neg_half[:], -0.5)
+        ident = const.tile([P, P], F32)
+        make_identity(nc, ident[:])
+
+        stats = const.tile([P, UNITS, STAT_CHUNKS, 6], F32)
+        pivot = const.tile([P, 6], F32)
+        sums = const.tile([P, 2, 2, GROUPS], F32)
+        gain = const.tile([P, COLS], F32)
+        beta = const.tile([P, COLS], F32)
+        bias = const.tile([P, CLASSES], F32)
+        for c in range(GROUPS):
+            for unit in range(UNITS):
+                zt = transpose_words(nc, zt_pool, ident, z_groups[c], unit)
+                if unit == SCALAR_UNIT:
+                    if c == 0:
+                        nc.vector.bn_stats(out=pivot[:], in_=as_values(zt)[:, 0:STAT_RUN])
+                    for e in range(2):
+                        for power, func in enumerate((ACT.Identity, ACT.Square)):
+                            unread = scratch.tile([P, GROUP_ROWS], BF16)
+                            nc.scalar.activation(
+                                out=unread[:],
+                                in_=as_pairs(zt)[:, :, e],
+                                func=func,
+                                bias=pivot[:, 3 * e + 1 : 3 * e + 2],
+                                scale=-1.0,
+                                accum_out=sums[:, power, e, c : c + 1],
+                            )
+                else:
+                    for s in range(2):
+                        nc.vector.bn_stats(
+                            out=stats[:, unit, 2 * c + s, :],
+                            in_=as_values(zt)[:, STAT_RUN * s : STAT_RUN * (s + 1)],
+                        )
+            if c == 0:
+                nc.vector.tensor_copy(out=gain[:], in_=gain_bf[:].rearrange("p g t -> p (g t)"))
+                nc.vector.tensor_copy(out=beta[:], in_=beta_bf[:].rearrange("p g t -> p (g t)"))
+                nc.vector.tensor_copy(out=bias[:], in_=bias_bf[:])
+
+        zts = {0: [transpose_words(nc, zt_pool, ident, z_groups[0], unit) for unit in range(UNITS)]}
+
+        mean_var = const.tile([P, COLS, 2], F32)
+        totals = const.tile([P, 2, 2], F32)
+        square = const.tile([P, 2], F32)
+        first = 2 * SCALAR_UNIT
+        nc.vector.tensor_reduce(out=totals[:], in_=sums[:], axis=AXIS.X, op=ALU.add)
+        nc.vector.tensor_scalar_mul(out=totals[:], in0=totals[:], scalar1=1.0 / ROWS)
+        nc.vector.tensor_sub(out=mean_var[:, first : first + 2, 0], in0=pivot[:, 1:6:3], in1=totals[:, 0, :])
+        nc.vector.tensor_mul(out=square[:], in0=totals[:, 0, :], in1=totals[:, 0, :])
+        nc.vector.tensor_sub(out=mean_var[:, first : first + 2, 1], in0=totals[:, 1, :], in1=square[:])
+        for unit in range(UNITS):
+            if unit != SCALAR_UNIT:
+                for e in range(2):
+                    nc.vector.bn_aggr(out=mean_var[:, 2 * unit + e, :], in_=stats[:, unit, :, 3 * e : 3 * e + 3])
+        var_eps = const.tile([P, COLS], F32)
+        rstd = const.tile([P, COLS], F32)
+        scale = const.tile([P, COLS], F32)
+        mean_scaled = const.tile([P, COLS], F32)
+        shift = const.tile([P, COLS], F32)
+        nc.vector.tensor_scalar_add(out=var_eps[:], in0=mean_var[:, :, 1], scalar1=BN_EPS)
+        nc.gpsimd.tensor_tensor(out=rstd[:], in0=var_eps[:], in1=neg_half[:], op=ALU.pow)
+        nc.vector.tensor_mul(out=scale[:], in0=rstd[:], in1=gain[:])
+        nc.vector.tensor_mul(out=mean_scaled[:], in0=mean_var[:, :, 0], in1=scale[:])
+        nc.vector.tensor_sub(out=shift[:], in0=beta[:], in1=mean_scaled[:])
+
+        neg_max = const.tile([P, TILES], F32)
+        sum_exp = const.tile([P, TILES], F32)
+        log_sum = const.tile([P, TILES], F32)
+        neg_shift = const.tile([P, TILES], F32)
+        planes_of, operand_of = {}, {}
+
+        def normalise(c):
+            planes = work.tile([P, PASSES, 4, GROUP_ROWS], BF16)
+            for unit in range(UNITS):
+                for e in range(2):
+                    col = 2 * unit + e
+                    nc.scalar.activation(
+                        out=planes[:, col // 4, col % 4, :],
+                        in_=as_pairs(zts[c][unit])[:, :, e],
+                        func=ACT.Relu,
+                        bias=shift[:, col : col + 1],
+                        scale=scale[:, col : col + 1],
+                    )
+            planes_of[c] = planes
+
+        def regroup(c):
+            grouped = work.tile([P, PASSES, GROUP_ROWS, 4], BF16, align_bytes=64)
+            for g in range(PASSES):
+                nc.vector.tensor_copy(
+                    out=grouped[:, g].rearrange("p (c i) t -> p c t i", i=4),
+                    in_=planes_of[c][:, g].rearrange("p t (c i) -> p c t i", i=4),
+                )
+            return grouped
+
+        def quantise(c, grouped):
+            codes = work.tile([P, PASSES, GROUP_ROWS], U32, align_bytes=64)
+            h_scales = work.tile([P, PASSES, GROUP_ROWS], U8, align_bytes=64)
+            nc.vector.quantize_mx(
+                out=codes[:].rearrange("p g r -> p (g r)").bitcast(FP8X4),
+                scales=h_scales[:].rearrange("p g r -> p (g r)"),
+                in_=grouped[:].rearrange("p g r t -> p (g r t)"),
+            )
+            operand_of[c] = (codes, h_scales)
+
+        def classify(c):
+            codes, h_scales = operand_of[c]
+            accs = []
+            for j in range(GROUP_TILES):
+                acc = acc_pool.tile([P, CLASSES], F32)
+                for g in range(PASSES):
+                    nc.tensor.matmul_mx(
+                        out=acc[:],
+                        lhsT=codes[:, g, P * j : P * (j + 1)].bitcast(FP8X4),
+                        lhsT_scale=h_scales[:, g, P * j : P * (j + 1)],
+                        rhs=w_words[:, g, :].bitcast(FP4X4),
+                        rhs_scale=w_scales[:, g, :],
+                        start=(g == 0),
+                        stop=(g == PASSES - 1),
+                    )
+                accs.append(acc)
+            return accs
+
+        def logits_and_max(c, accs):
+            for j in range(GROUP_TILES):
+                col = GROUP_TILES * c + j
+                nc.vector.tensor_tensor(out=z_groups[c][:, j, :], in0=accs[j][:], in1=bias[:], op=ALU.add)
+                nc.vector.tensor_reduce(
+                    out=neg_max[:, col : col + 1], in_=z_groups[c][:, j, :], axis=AXIS.X, op=ALU.max, negate=True
+                )
+
+        def sum_of_exp(c):
+            for j in range(GROUP_TILES):
+                col = GROUP_TILES * c + j
+                unread = scratch.tile([P, CLASSES], BF16)
+                nc.scalar.activation(
+                    out=unread[:],
+                    in_=z_groups[c][:, j, :],
+                    func=ACT.Exp,
+                    bias=neg_max[:, col : col + 1],
+                    scale=1.0,
+                    accum_out=sum_exp[:, col : col + 1],
+                )
+
+        def finish(c_from, c_to):
+            lo, hi = GROUP_TILES * c_from, GROUP_TILES * c_to
+            nc.scalar.activation(out=log_sum[:, lo:hi], in_=sum_exp[:, lo:hi], func=ACT.Ln)
+            nc.gpsimd.tensor_tensor(out=neg_shift[:, lo:hi], in0=neg_max[:, lo:hi], in1=log_sum[:, lo:hi], op=ALU.subtract)
+            for c in range(c_from, c_to):
+                for j in range(GROUP_TILES):
+                    col = GROUP_TILES * c + j
+                    if c_to == GROUPS:
+                        nc.vector.tensor_scalar_add(
+                            out=z_groups[c][:, j, :], in0=z_groups[c][:, j, :], scalar1=neg_shift[:, col : col + 1]
+                        )
+                    else:
+                        nc.gpsimd.tensor_scalar(
+                            out=z_groups[c][:, j, :],
+                            in0=z_groups[c][:, j, :],
+                            scalar1=1.0,
+                            scalar2=neg_shift[:, col : col + 1],
+                            op0=ALU.mult,
+                            op1=ALU.add,
+                        )
+                nc.sync.dma_start(out=out_rows[:, GROUP_TILES * c : GROUP_TILES * (c + 1), :], in_=z_groups[c][:])
+
+        for k in range(GROUPS + 2):
+            if k >= 2:
+                accs = classify(k - 2)
+            if k < GROUPS:
+                normalise(k)
+            if k + 1 < GROUPS:
+                zts[k + 1] = [transpose_words(nc, zt_pool, ident, z_groups[k + 1], unit) for unit in range(UNITS)]
+            if 1 <= k <= GROUPS:
+                grouped = regroup(k - 1)
+            if k >= 2:
+                logits_and_max(k - 2, accs)
+                sum_of_exp(k - 2)
+            if 1 <= k <= GROUPS:
+                quantise(k - 1, grouped)
+            if k >= 2 and (k - 1) % LN_GROUPS == 0:
+                finish(k - 1 - LN_GROUPS, k - 1)

@@ -212,12 +212,18 @@ def tile_binarymlp_pb_t_kernel(tc, z2, g2, beta2, W3_words, W3_scales, b3, out):
             return accs
 
         def logits_and_max(c, accs):
-            for j in range(GROUP_TILES):
-                col = GROUP_TILES * c + j
-                nc.vector.tensor_tensor(out=z_groups[c][:, j, :], in0=accs[j][:], in1=bias[:], op=ALU.add)
-                nc.vector.tensor_reduce(
-                    out=neg_max[:, col : col + 1], in_=z_groups[c][:, j, :], axis=AXIS.X, op=ALU.max, negate=True
-                )
+            for j in range(GROUP_TILES + 1):
+                if j < GROUP_TILES:
+                    nc.vector.tensor_tensor(out=z_groups[c][:, j, :], in0=accs[j][:], in1=bias[:], op=ALU.add)
+                if j >= 1:
+                    col = GROUP_TILES * c + j - 1
+                    nc.vector.tensor_reduce(
+                        out=neg_max[:, col : col + 1],
+                        in_=z_groups[c][:, j - 1, :],
+                        axis=AXIS.X,
+                        op=ALU.max,
+                        negate=True,
+                    )
 
         def sum_of_exp(c):
             for j in range(GROUP_TILES):
@@ -254,19 +260,20 @@ def tile_binarymlp_pb_t_kernel(tc, z2, g2, beta2, W3_words, W3_scales, b3, out):
                         )
                 nc.sync.dma_start(out=out_rows[:, GROUP_TILES * c : GROUP_TILES * (c + 1), :], in_=z_groups[c][:])
 
+        accs_of, grouped_of = {}, {}
         for k in range(GROUPS + 2):
             if k >= 2:
-                accs = classify(k - 2)
+                logits_and_max(k - 2, accs_of[k - 2])
             if k < GROUPS:
                 normalise(k)
+            if k >= 2:
+                sum_of_exp(k - 2)
             if k + 1 < GROUPS:
                 zts[k + 1] = [transpose_words(nc, zt_pool, ident, z_groups[k + 1], unit) for unit in range(UNITS)]
             if 1 <= k <= GROUPS:
-                grouped = regroup(k - 1)
-            if k >= 2:
-                logits_and_max(k - 2, accs)
-                sum_of_exp(k - 2)
-            if 1 <= k <= GROUPS:
-                quantise(k - 1, grouped)
+                quantise(k - 1, grouped_of[k - 1])
+                accs_of[k - 1] = classify(k - 1)
+            if k < GROUPS:
+                grouped_of[k] = regroup(k)
             if k >= 2 and (k - 1) % LN_GROUPS == 0:
                 finish(k - 1 - LN_GROUPS, k - 1)

@@ -133,31 +133,43 @@ def tile_binarymlp_pb_t_kernel(tc, z2, g2, beta2, W3_words, W3_scales, b3, out):
         mean_var = const.tile([P, COLS, 2], F32)
         totals = const.tile([P, 2, 2], F32)
         square = const.tile([P, 2], F32)
-        first = 2 * SCALAR_UNIT
-        nc.vector.tensor_reduce(out=totals[:], in_=sums[:], axis=AXIS.X, op=ALU.add)
-        nc.vector.tensor_scalar_mul(out=totals[:], in0=totals[:], scalar1=1.0 / ROWS)
-        nc.vector.tensor_sub(out=mean_var[:, first : first + 2, 0], in0=pivot[:, 1:6:3], in1=totals[:, 0, :])
-        nc.vector.tensor_mul(out=square[:], in0=totals[:, 0, :], in1=totals[:, 0, :])
-        nc.vector.tensor_sub(out=mean_var[:, first : first + 2, 1], in0=totals[:, 1, :], in1=square[:])
-        for unit in range(UNITS):
-            if unit != SCALAR_UNIT:
-                for e in range(2):
-                    nc.vector.bn_aggr(out=mean_var[:, 2 * unit + e, :], in_=stats[:, unit, :, 3 * e : 3 * e + 3])
         var_eps = const.tile([P, COLS], F32)
         rstd = const.tile([P, COLS], F32)
         scale = const.tile([P, COLS], F32)
         mean_scaled = const.tile([P, COLS], F32)
         shift = const.tile([P, COLS], F32)
-        nc.vector.tensor_scalar_add(out=var_eps[:], in0=mean_var[:, :, 1], scalar1=BN_EPS)
-        nc.gpsimd.tensor_tensor(out=rstd[:], in0=var_eps[:], in1=neg_half[:], op=ALU.pow)
-        nc.vector.tensor_mul(out=scale[:], in0=rstd[:], in1=gain[:])
-        nc.vector.tensor_mul(out=mean_scaled[:], in0=mean_var[:, :, 0], in1=scale[:])
-        nc.vector.tensor_sub(out=shift[:], in0=beta[:], in1=mean_scaled[:])
+        nc.vector.tensor_reduce(out=totals[:], in_=sums[:], axis=AXIS.X, op=ALU.add)
+        for g in range(PASSES):
+            for unit in range(2 * g, 2 * g + 2):
+                if unit != SCALAR_UNIT:
+                    for e in range(2):
+                        nc.vector.bn_aggr(out=mean_var[:, 2 * unit + e, :], in_=stats[:, unit, :, 3 * e : 3 * e + 3])
+            if SCALAR_UNIT // 2 == g:
+                own = slice(2 * SCALAR_UNIT, 2 * SCALAR_UNIT + 2)
+                nc.vector.scalar_tensor_tensor(
+                    out=mean_var[:, own, 0], in0=totals[:, 0, :], scalar=-1.0 / ROWS, in1=pivot[:, 1:6:3],
+                    op0=ALU.mult, op1=ALU.add,
+                )
+                nc.vector.scalar_tensor_tensor(
+                    out=square[:], in0=totals[:, 0, :], scalar=1.0 / (ROWS * ROWS), in1=totals[:, 0, :],
+                    op0=ALU.mult, op1=ALU.mult,
+                )
+                nc.vector.scalar_tensor_tensor(
+                    out=mean_var[:, own, 1], in0=totals[:, 1, :], scalar=1.0 / ROWS, in1=square[:],
+                    op0=ALU.mult, op1=ALU.subtract,
+                )
+            cols = slice(4 * g, 4 * g + 4)
+            nc.vector.tensor_scalar_add(out=var_eps[:, cols], in0=mean_var[:, cols, 1], scalar1=BN_EPS)
+            nc.gpsimd.tensor_tensor(out=rstd[:, cols], in0=var_eps[:, cols], in1=neg_half[:, cols], op=ALU.pow)
+        for g in range(PASSES):
+            cols = slice(4 * g, 4 * g + 4)
+            nc.vector.tensor_mul(out=scale[:, cols], in0=rstd[:, cols], in1=gain[:, cols])
+            nc.vector.tensor_mul(out=mean_scaled[:, cols], in0=mean_var[:, cols, 0], in1=scale[:, cols])
+            nc.vector.tensor_sub(out=shift[:, cols], in0=beta[:, cols], in1=mean_scaled[:, cols])
 
         neg_max = const.tile([P, TILES], F32)
         sum_exp = const.tile([P, TILES], F32)
         log_sum = const.tile([P, TILES], F32)
-        neg_shift = const.tile([P, TILES], F32)
         planes_of, operand_of = {}, {}
 
         def normalise(c):
@@ -239,28 +251,26 @@ def tile_binarymlp_pb_t_kernel(tc, z2, g2, beta2, W3_words, W3_scales, b3, out):
                 )
 
         def finish(c_from, c_to):
+            engine = nc.vector if c_to == GROUPS else nc.gpsimd
             lo, hi = GROUP_TILES * c_from, GROUP_TILES * c_to
             nc.scalar.activation(out=log_sum[:, lo:hi], in_=sum_exp[:, lo:hi], func=ACT.Ln)
-            nc.gpsimd.tensor_tensor(out=neg_shift[:, lo:hi], in0=neg_max[:, lo:hi], in1=log_sum[:, lo:hi], op=ALU.subtract)
+            neg_shift = work.tile([P, LN_GROUPS * GROUP_TILES], F32)
+            engine.tensor_tensor(out=neg_shift[:, 0 : hi - lo], in0=neg_max[:, lo:hi], in1=log_sum[:, lo:hi], op=ALU.subtract)
             for c in range(c_from, c_to):
                 for j in range(GROUP_TILES):
-                    col = GROUP_TILES * c + j
-                    if c_to == GROUPS:
-                        nc.vector.tensor_scalar_add(
-                            out=z_groups[c][:, j, :], in0=z_groups[c][:, j, :], scalar1=neg_shift[:, col : col + 1]
-                        )
-                    else:
-                        nc.gpsimd.tensor_scalar(
-                            out=z_groups[c][:, j, :],
-                            in0=z_groups[c][:, j, :],
-                            scalar1=1.0,
-                            scalar2=neg_shift[:, col : col + 1],
-                            op0=ALU.mult,
-                            op1=ALU.add,
-                        )
+                    col = GROUP_TILES * c + j - lo
+                    engine.tensor_scalar(
+                        out=z_groups[c][:, j, :],
+                        in0=z_groups[c][:, j, :],
+                        scalar1=1.0,
+                        scalar2=neg_shift[:, col : col + 1],
+                        op0=ALU.mult,
+                        op1=ALU.add,
+                    )
                 nc.sync.dma_start(out=out_rows[:, GROUP_TILES * c : GROUP_TILES * (c + 1), :], in_=z_groups[c][:])
 
         accs_of, grouped_of = {}, {}
+        finished = 0
         for k in range(GROUPS + 2):
             if k >= 2:
                 logits_and_max(k - 2, accs_of[k - 2])
@@ -275,5 +285,6 @@ def tile_binarymlp_pb_t_kernel(tc, z2, g2, beta2, W3_words, W3_scales, b3, out):
                 accs_of[k - 1] = classify(k - 1)
             if k < GROUPS:
                 grouped_of[k] = regroup(k)
-            if k >= 2 and (k - 1) % LN_GROUPS == 0:
-                finish(k - 1 - LN_GROUPS, k - 1)
+            if k >= 2 and ((k - 1) % LN_GROUPS == 0 or k >= GROUPS):
+                finish(finished, k - 1)
+                finished = k - 1

@@ -27,7 +27,11 @@ GROUP_ROWS = GROUP_TILES * P
 LN_GROUPS = 4
 STAT_RUN = 512
 STAT_CHUNKS = 2 * ROWS // STAT_RUN
-SCALAR_UNIT = 0
+VECTOR_UNITS = (0, 1)
+SCALAR_UNIT = 2
+TENSOR_UNIT = 3
+PAD = 8
+PITCH = CLASSES + PAD
 
 FLOPS = 2 * ROWS * FEATURES * CLASSES
 
@@ -38,6 +42,19 @@ def transpose_words(nc, zt_pool, ident, z_group, unit):
     for j in range(GROUP_TILES):
         nc.tensor.transpose(zt[:, j, :], z_group[:, j, 256 * g + u : 256 * (g + 1) : 2], ident[:])
     return zt
+
+
+def add_products(nc, gram, z_group, j, e, start, stop):
+    g, u = divmod(TENSOR_UNIT, 2)
+    first = 4 * P * g + 2 * u + e
+    values = z_group[:, j, :].bitcast(BF16)
+    nc.tensor.matmul(
+        out=gram[:, 0 : P + 1],
+        lhsT=values[:, first : first + 4 * P : 4],
+        rhs=values[:, first : first + 4 * P + 1 : 4],
+        start=start,
+        stop=stop,
+    )
 
 
 def as_values(zt):
@@ -64,9 +81,10 @@ def tile_binarymlp_pb_t_kernel(tc, z2, g2, beta2, W3_words, W3_scales, b3, out):
 
         z_groups = []
         for c in range(GROUPS):
-            z_group = resident.tile([P, GROUP_TILES, CLASSES], F32, name="z_group%d" % c)
+            z_group = resident.tile([P, GROUP_TILES, PITCH], F32, name="z_group%d" % c)
+            nc.vector.memset(z_group[:, :, CLASSES:PITCH].bitcast(BF16), 1.0)
             nc.sync.dma_start(
-                out=z_group[:].bitcast(BF16),
+                out=z_group[:, :, 0:CLASSES].bitcast(BF16),
                 in_=z_rows[:, GROUP_TILES * c : GROUP_TILES * (c + 1), :],
             )
             z_groups.append(z_group)
@@ -100,8 +118,9 @@ def tile_binarymlp_pb_t_kernel(tc, z2, g2, beta2, W3_words, W3_scales, b3, out):
         gain = const.tile([P, COLS], F32)
         beta = const.tile([P, COLS], F32)
         bias = const.tile([P, CLASSES], F32)
+        grams = [acc_pool.tile([P, CLASSES], F32, name="acc") for e in range(2)]
         for c in range(GROUPS):
-            for unit in range(UNITS):
+            for unit in (SCALAR_UNIT,) + VECTOR_UNITS:
                 zt = transpose_words(nc, zt_pool, ident, z_groups[c], unit)
                 if unit == SCALAR_UNIT:
                     if c == 0:
@@ -123,6 +142,12 @@ def tile_binarymlp_pb_t_kernel(tc, z2, g2, beta2, W3_words, W3_scales, b3, out):
                             out=stats[:, unit, 2 * c + s, :],
                             in_=as_values(zt)[:, STAT_RUN * s : STAT_RUN * (s + 1)],
                         )
+            for j in range(GROUP_TILES):
+                for e in range(2):
+                    add_products(
+                        nc, grams[e], z_groups[c], j, e,
+                        start=(c == 0 and j == 0), stop=(c == GROUPS - 1 and j == GROUP_TILES - 1),
+                    )
             if c == 0:
                 nc.vector.tensor_copy(out=gain[:], in_=gain_bf[:].rearrange("p g t -> p (g t)"))
                 nc.vector.tensor_copy(out=beta[:], in_=beta_bf[:].rearrange("p g t -> p (g t)"))
@@ -138,13 +163,27 @@ def tile_binarymlp_pb_t_kernel(tc, z2, g2, beta2, W3_words, W3_scales, b3, out):
         scale = const.tile([P, COLS], F32)
         mean_scaled = const.tile([P, COLS], F32)
         shift = const.tile([P, COLS], F32)
-        nc.vector.tensor_reduce(out=totals[:], in_=sums[:], axis=AXIS.X, op=ALU.add)
+        diagonal = const.tile([P, 2, P], F32)
+        mean_square = const.tile([P, 2], F32)
         for g in range(PASSES):
             for unit in range(2 * g, 2 * g + 2):
-                if unit != SCALAR_UNIT:
+                if unit in VECTOR_UNITS:
                     for e in range(2):
                         nc.vector.bn_aggr(out=mean_var[:, 2 * unit + e, :], in_=stats[:, unit, :, 3 * e : 3 * e + 3])
+            if TENSOR_UNIT // 2 == g:
+                own = slice(2 * TENSOR_UNIT, 2 * TENSOR_UNIT + 2)
+                for e in range(2):
+                    nc.vector.scalar_tensor_tensor(
+                        out=diagonal[:, e, :], in0=grams[e][:, 0:P], scalar=1.0 / ROWS, in1=ident[:],
+                        op0=ALU.mult, op1=ALU.mult, accum_out=mean_square[:, e : e + 1],
+                    )
+                    nc.vector.tensor_scalar_mul(
+                        out=mean_var[:, 2 * TENSOR_UNIT + e, 0:1], in0=grams[e][:, P : P + 1], scalar1=1.0 / ROWS
+                    )
+                nc.vector.tensor_mul(out=square[:], in0=mean_var[:, own, 0], in1=mean_var[:, own, 0])
+                nc.vector.tensor_sub(out=mean_var[:, own, 1], in0=mean_square[:], in1=square[:])
             if SCALAR_UNIT // 2 == g:
+                nc.vector.tensor_reduce(out=totals[:], in_=sums[:], axis=AXIS.X, op=ALU.add)
                 own = slice(2 * SCALAR_UNIT, 2 * SCALAR_UNIT + 2)
                 nc.vector.scalar_tensor_tensor(
                     out=mean_var[:, own, 0], in0=totals[:, 0, :], scalar=-1.0 / ROWS, in1=pivot[:, 1:6:3],
@@ -209,7 +248,7 @@ def tile_binarymlp_pb_t_kernel(tc, z2, g2, beta2, W3_words, W3_scales, b3, out):
             codes, h_scales = operand_of[c]
             accs = []
             for j in range(GROUP_TILES):
-                acc = acc_pool.tile([P, CLASSES], F32)
+                acc = acc_pool.tile([P, CLASSES], F32, name="acc")
                 for g in range(PASSES):
                     nc.tensor.matmul_mx(
                         out=acc[:],
@@ -226,12 +265,12 @@ def tile_binarymlp_pb_t_kernel(tc, z2, g2, beta2, W3_words, W3_scales, b3, out):
         def logits_and_max(c, accs):
             for j in range(GROUP_TILES + 1):
                 if j < GROUP_TILES:
-                    nc.vector.tensor_tensor(out=z_groups[c][:, j, :], in0=accs[j][:], in1=bias[:], op=ALU.add)
+                    nc.vector.tensor_tensor(out=z_groups[c][:, j, 0:CLASSES], in0=accs[j][:], in1=bias[:], op=ALU.add)
                 if j >= 1:
                     col = GROUP_TILES * c + j - 1
                     nc.vector.tensor_reduce(
                         out=neg_max[:, col : col + 1],
-                        in_=z_groups[c][:, j - 1, :],
+                        in_=z_groups[c][:, j - 1, 0:CLASSES],
                         axis=AXIS.X,
                         op=ALU.max,
                         negate=True,
@@ -243,7 +282,7 @@ def tile_binarymlp_pb_t_kernel(tc, z2, g2, beta2, W3_words, W3_scales, b3, out):
                 unread = scratch.tile([P, CLASSES], BF16)
                 nc.scalar.activation(
                     out=unread[:],
-                    in_=z_groups[c][:, j, :],
+                    in_=z_groups[c][:, j, 0:CLASSES],
                     func=ACT.Exp,
                     bias=neg_max[:, col : col + 1],
                     scale=1.0,
@@ -260,14 +299,14 @@ def tile_binarymlp_pb_t_kernel(tc, z2, g2, beta2, W3_words, W3_scales, b3, out):
                 for j in range(GROUP_TILES):
                     col = GROUP_TILES * c + j - lo
                     engine.tensor_scalar(
-                        out=z_groups[c][:, j, :],
-                        in0=z_groups[c][:, j, :],
+                        out=z_groups[c][:, j, 0:CLASSES],
+                        in0=z_groups[c][:, j, 0:CLASSES],
                         scalar1=1.0,
                         scalar2=neg_shift[:, col : col + 1],
                         op0=ALU.mult,
                         op1=ALU.add,
                     )
-                nc.sync.dma_start(out=out_rows[:, GROUP_TILES * c : GROUP_TILES * (c + 1), :], in_=z_groups[c][:])
+                nc.sync.dma_start(out=out_rows[:, GROUP_TILES * c : GROUP_TILES * (c + 1), :], in_=z_groups[c][:, :, 0:CLASSES])
 
         accs_of, grouped_of = {}, {}
         finished = 0

@@ -25,12 +25,13 @@ GROUP_TILES = 4
 GROUPS = TILES // GROUP_TILES
 GROUP_ROWS = GROUP_TILES * P
 LN_GROUPS = 4
+LN_AFTER = (4, 8, 12, 14, 15, 16)
 STAT_RUN = 512
 STAT_CHUNKS = 2 * ROWS // STAT_RUN
 VECTOR_UNITS = (0, 1)
 SCALAR_UNIT = 2
 TENSOR_UNIT = 3
-PAD = 8
+PAD = 64
 PITCH = CLASSES + PAD
 
 FLOPS = 2 * ROWS * FEATURES * CLASSES
@@ -81,12 +82,13 @@ def tile_binarymlp_pb_t_kernel(tc, z2, g2, beta2, W3_words, W3_scales, b3, out):
 
         z_groups = []
         for c in range(GROUPS):
-            z_group = resident.tile([P, GROUP_TILES, PITCH], F32, name="z_group%d" % c)
-            nc.vector.memset(z_group[:, :, CLASSES:PITCH].bitcast(BF16), 1.0)
-            nc.sync.dma_start(
-                out=z_group[:, :, 0:CLASSES].bitcast(BF16),
-                in_=z_rows[:, GROUP_TILES * c : GROUP_TILES * (c + 1), :],
-            )
+            z_group = resident.tile([P, GROUP_TILES, PITCH], F32, name="z_group%d" % c, align_bytes=256)
+            nc.vector.memset(z_group[:, :, CLASSES : CLASSES + 8].bitcast(BF16), 1.0)
+            for j0, j1 in [(j, j + 1) for j in range(GROUP_TILES)] if c == 0 else [(0, GROUP_TILES)]:
+                nc.sync.dma_start(
+                    out=z_group[:, j0:j1, 0:CLASSES].bitcast(BF16),
+                    in_=z_rows[:, GROUP_TILES * c + j0 : GROUP_TILES * c + j1, :],
+                )
             z_groups.append(z_group)
 
         w_scales = const.tile([P, PASSES, CLASSES], U8, align_bytes=64)
@@ -244,11 +246,11 @@ def tile_binarymlp_pb_t_kernel(tc, z2, g2, beta2, W3_words, W3_scales, b3, out):
             )
             operand_of[c] = (codes, h_scales)
 
-        def classify(c):
+        def classify(c, pool, tag):
             codes, h_scales = operand_of[c]
             accs = []
             for j in range(GROUP_TILES):
-                acc = acc_pool.tile([P, CLASSES], F32, name="acc")
+                acc = pool.tile([P, CLASSES], F32, name=tag)
                 for g in range(PASSES):
                     nc.tensor.matmul_mx(
                         out=acc[:],
@@ -289,15 +291,17 @@ def tile_binarymlp_pb_t_kernel(tc, z2, g2, beta2, W3_words, W3_scales, b3, out):
                     accum_out=sum_exp[:, col : col + 1],
                 )
 
-        def finish(c_from, c_to):
-            engine = nc.vector if c_to == GROUPS else nc.gpsimd
+        def shifts(c_from, c_to, engine):
             lo, hi = GROUP_TILES * c_from, GROUP_TILES * c_to
             nc.scalar.activation(out=log_sum[:, lo:hi], in_=sum_exp[:, lo:hi], func=ACT.Ln)
             neg_shift = work.tile([P, LN_GROUPS * GROUP_TILES], F32)
             engine.tensor_tensor(out=neg_shift[:, 0 : hi - lo], in0=neg_max[:, lo:hi], in1=log_sum[:, lo:hi], op=ALU.subtract)
+            return neg_shift
+
+        def subtract_and_store(neg_shift, c_first, c_from, c_to, engine):
             for c in range(c_from, c_to):
                 for j in range(GROUP_TILES):
-                    col = GROUP_TILES * c + j - lo
+                    col = GROUP_TILES * (c - c_first) + j
                     engine.tensor_scalar(
                         out=z_groups[c][:, j, 0:CLASSES],
                         in0=z_groups[c][:, j, 0:CLASSES],
@@ -311,6 +315,9 @@ def tile_binarymlp_pb_t_kernel(tc, z2, g2, beta2, W3_words, W3_scales, b3, out):
         accs_of, grouped_of = {}, {}
         finished = 0
         for k in range(GROUPS + 2):
+            if k == GROUPS:
+                quantise(k - 1, grouped_of[k - 1])
+                accs_of[k - 1] = classify(k - 1, zt_pool, "zt")
             if k >= 2:
                 logits_and_max(k - 2, accs_of[k - 2])
             if k < GROUPS:
@@ -319,11 +326,12 @@ def tile_binarymlp_pb_t_kernel(tc, z2, g2, beta2, W3_words, W3_scales, b3, out):
                 sum_of_exp(k - 2)
             if k + 1 < GROUPS:
                 zts[k + 1] = [transpose_words(nc, zt_pool, ident, z_groups[k + 1], unit) for unit in range(UNITS)]
-            if 1 <= k <= GROUPS:
+            if 1 <= k < GROUPS:
                 quantise(k - 1, grouped_of[k - 1])
-                accs_of[k - 1] = classify(k - 1)
+                accs_of[k - 1] = classify(k - 1, acc_pool, "acc")
             if k < GROUPS:
                 grouped_of[k] = regroup(k)
-            if k >= 2 and ((k - 1) % LN_GROUPS == 0 or k >= GROUPS):
-                finish(finished, k - 1)
+            if k - 1 in LN_AFTER:
+                engine = nc.vector if k - 1 == GROUPS else nc.gpsimd
+                subtract_and_store(shifts(finished, k - 1, engine), finished, finished, k - 1, engine)
                 finished = k - 1

@@ -31,7 +31,7 @@ STAT_CHUNKS = 2 * ROWS // STAT_RUN
 VECTOR_UNITS = (0, 1)
 SCALAR_UNIT = 2
 TENSOR_UNIT = 3
-PAD = 64
+PAD = 8
 PITCH = CLASSES + PAD
 
 FLOPS = 2 * ROWS * FEATURES * CLASSES
@@ -82,13 +82,12 @@ def tile_binarymlp_pb_t_kernel(tc, z2, g2, beta2, W3_words, W3_scales, b3, out):
 
         z_groups = []
         for c in range(GROUPS):
-            z_group = resident.tile([P, GROUP_TILES, PITCH], F32, name="z_group%d" % c, align_bytes=256)
+            z_group = resident.tile([P, GROUP_TILES, PITCH], F32, name="z_group%d" % c)
             nc.vector.memset(z_group[:, :, CLASSES : CLASSES + 8].bitcast(BF16), 1.0)
-            for j0, j1 in [(j, j + 1) for j in range(GROUP_TILES)] if c == 0 else [(0, GROUP_TILES)]:
-                nc.sync.dma_start(
-                    out=z_group[:, j0:j1, 0:CLASSES].bitcast(BF16),
-                    in_=z_rows[:, GROUP_TILES * c + j0 : GROUP_TILES * c + j1, :],
-                )
+            nc.sync.dma_start(
+                out=z_group[:, :, 0:CLASSES].bitcast(BF16),
+                in_=z_rows[:, GROUP_TILES * c : GROUP_TILES * (c + 1), :],
+            )
             z_groups.append(z_group)
 
         w_scales = const.tile([P, PASSES, CLASSES], U8, align_bytes=64)

@@ -230,8 +230,8 @@ def tile_binarymlp_pb_t_kernel(tc, z2, g2, beta2, W3_words, W3_scales, b3, out):
             grouped = work.tile([P, PASSES, GROUP_ROWS, 4], BF16, align_bytes=64)
             for g in range(PASSES):
                 nc.vector.tensor_copy(
-                    out=grouped[:, g].rearrange("p (c i) t -> p c t i", i=4),
-                    in_=planes_of[c][:, g].rearrange("p t (c i) -> p c t i", i=4),
+                    out=grouped[:, g].rearrange("p (c i) t -> p c t i", i=8),
+                    in_=planes_of[c][:, g].rearrange("p t (c i) -> p c t i", i=8),
                 )
             return grouped
 

@@ -28,9 +28,11 @@ LN_GROUPS = 4
 LN_AFTER = (4, 8, 12, 14, 15, 16)
 STAT_RUN = 512
 STAT_CHUNKS = 2 * ROWS // STAT_RUN
-VECTOR_UNITS = (0, 1)
-SCALAR_UNIT = 2
-TENSOR_UNIT = 3
+BLOCKS = FEATURES // (2 * P)
+HALF = P // 2
+VECTOR_BLOCKS = (0, 1)
+SCALAR_BLOCK = 2
+TENSOR_BLOCK = 3
 PAD = 8
 PITCH = CLASSES + PAD
 
@@ -39,20 +41,26 @@ FLOPS = 2 * ROWS * FEATURES * CLASSES
 
 def transpose_words(nc, zt_pool, ident, z_group, unit):
     g, u = divmod(unit, 2)
-    zt = zt_pool.tile([P, GROUP_TILES, P], F32)
+    zt = zt_pool.tile([P, GROUP_TILES, P], F32, name="zt")
     for j in range(GROUP_TILES):
         nc.tensor.transpose(zt[:, j, :], z_group[:, j, 256 * g + u : 256 * (g + 1) : 2], ident[:])
     return zt
 
 
+def transpose_block(nc, zt_pool, ident, z_group, b):
+    zt = zt_pool.tile([P, GROUP_TILES, P], F32, name="zt")
+    for j in range(GROUP_TILES):
+        nc.tensor.transpose(zt[:, j, :], z_group[:, j, P * b : P * (b + 1)], ident[:])
+    return zt
+
+
 def add_products(nc, gram, z_group, j, e, start, stop):
-    g, u = divmod(TENSOR_UNIT, 2)
-    first = 4 * P * g + 2 * u + e
+    first = 2 * P * TENSOR_BLOCK + e
     values = z_group[:, j, :].bitcast(BF16)
     nc.tensor.matmul(
         out=gram[:, 0 : P + 1],
-        lhsT=values[:, first : first + 4 * P : 4],
-        rhs=values[:, first : first + 4 * P + 1 : 4],
+        lhsT=values[:, first : first + 2 * P : 2],
+        rhs=values[:, first : first + 2 * P + 1 : 2],
         start=start,
         stop=stop,
     )
@@ -113,17 +121,21 @@ def tile_binarymlp_pb_t_kernel(tc, z2, g2, beta2, W3_words, W3_scales, b3, out):
         ident = const.tile([P, P], F32)
         make_identity(nc, ident[:])
 
-        stats = const.tile([P, UNITS, STAT_CHUNKS, 6], F32)
+        stats = const.tile([P, len(VECTOR_BLOCKS), STAT_CHUNKS, 6], F32)
         pivot = const.tile([P, 6], F32)
         sums = const.tile([P, 2, 2, GROUPS], F32)
         gain = const.tile([P, COLS], F32)
         beta = const.tile([P, COLS], F32)
         bias = const.tile([P, CLASSES], F32)
+        moments = const.tile([P, P], F32)
+        nc.vector.memset(moments[:], 0.0)
+        turned = const.tile([P, 2, P], F32)
+        nc.vector.memset(turned[:], 0.0)
         grams = [acc_pool.tile([P, CLASSES], F32, name="acc") for e in range(2)]
         for c in range(GROUPS):
-            for unit in (SCALAR_UNIT,) + VECTOR_UNITS:
-                zt = transpose_words(nc, zt_pool, ident, z_groups[c], unit)
-                if unit == SCALAR_UNIT:
+            for b in (SCALAR_BLOCK,) + VECTOR_BLOCKS:
+                zt = transpose_block(nc, zt_pool, ident, z_groups[c], b)
+                if b == SCALAR_BLOCK:
                     if c == 0:
                         nc.vector.bn_stats(out=pivot[:], in_=as_values(zt)[:, 0:STAT_RUN])
                     for e in range(2):
@@ -140,7 +152,7 @@ def tile_binarymlp_pb_t_kernel(tc, z2, g2, beta2, W3_words, W3_scales, b3, out):
                 else:
                     for s in range(2):
                         nc.vector.bn_stats(
-                            out=stats[:, unit, 2 * c + s, :],
+                            out=stats[:, b, 2 * c + s, :],
                             in_=as_values(zt)[:, STAT_RUN * s : STAT_RUN * (s + 1)],
                         )
             for j in range(GROUP_TILES):
@@ -154,57 +166,83 @@ def tile_binarymlp_pb_t_kernel(tc, z2, g2, beta2, W3_words, W3_scales, b3, out):
                 nc.vector.tensor_copy(out=beta[:], in_=beta_bf[:].rearrange("p g t -> p (g t)"))
                 nc.vector.tensor_copy(out=bias[:], in_=bias_bf[:])
 
-        zts = {0: [transpose_words(nc, zt_pool, ident, z_groups[0], unit) for unit in range(UNITS)]}
+        zts = {0: [transpose_words(nc, zt_pool, ident, z_groups[0], unit) for unit in range(UNITS - 1)]}
 
-        mean_var = const.tile([P, COLS, 2], F32)
         totals = const.tile([P, 2, 2], F32)
         square = const.tile([P, 2], F32)
+        diagonal = const.tile([P, 2, P], F32)
+        mean_square = const.tile([P, 2], F32)
+
+        def columns(b):
+            g, h = divmod(b, 2)
+            return moments[:, 32 * h + 4 * g : 32 * h + 4 * g + 4].rearrange("p (e m) -> p e m", m=2)
+
+        own = columns(TENSOR_BLOCK)
+        for e in range(2):
+            nc.vector.scalar_tensor_tensor(
+                out=diagonal[:, e, :], in0=grams[e][:, 0:P], scalar=1.0 / ROWS, in1=ident[:],
+                op0=ALU.mult, op1=ALU.mult, accum_out=mean_square[:, e : e + 1],
+            )
+            nc.vector.tensor_scalar_mul(out=own[:, e, 0:1], in0=grams[e][:, P : P + 1], scalar1=1.0 / ROWS)
+        nc.vector.tensor_mul(out=square[:], in0=own[:, :, 0], in1=own[:, :, 0])
+        for b in VECTOR_BLOCKS:
+            for e in range(2):
+                nc.vector.bn_aggr(out=columns(b)[:, e, :], in_=stats[:, b, :, 3 * e : 3 * e + 3])
+        nc.vector.tensor_sub(out=own[:, :, 1], in0=mean_square[:], in1=square[:])
+        nc.vector.tensor_reduce(out=totals[:], in_=sums[:], axis=AXIS.X, op=ALU.add)
+        own = columns(SCALAR_BLOCK)
+        nc.vector.scalar_tensor_tensor(
+            out=own[:, :, 0], in0=totals[:, 0, :], scalar=-1.0 / ROWS, in1=pivot[:, 1:6:3],
+            op0=ALU.mult, op1=ALU.add,
+        )
+        nc.vector.scalar_tensor_tensor(
+            out=square[:], in0=totals[:, 0, :], scalar=1.0 / (ROWS * ROWS), in1=totals[:, 0, :],
+            op0=ALU.mult, op1=ALU.mult,
+        )
+        nc.vector.scalar_tensor_tensor(
+            out=own[:, :, 1], in0=totals[:, 1, :], scalar=1.0 / ROWS, in1=square[:],
+            op0=ALU.mult, op1=ALU.subtract,
+        )
+
+        first_turn = acc_pool.tile([P, CLASSES], F32, name="acc")
+        nc.tensor.transpose(first_turn[:, 0:P], moments[:], ident[:])
+        nc.vector.tensor_copy(
+            out=turned[0:HALF, :, :], in_=first_turn[0:HALF, 0:P].unsqueeze(1).to_broadcast([HALF, 2, P])
+        )
+        second_turn = acc_pool.tile([P, CLASSES], F32, name="acc")
+        for u in range(2):
+            nc.tensor.transpose(
+                second_turn[:, P * u : P * (u + 1)], turned[:].rearrange("p h q -> p (h q)")[:, u : 2 * P : 2], ident[:]
+            )
+        zts[0].append(transpose_words(nc, zt_pool, ident, z_groups[0], UNITS - 1))
+
+        mean = const.tile([P, COLS], F32)
         var_eps = const.tile([P, COLS], F32)
         rstd = const.tile([P, COLS], F32)
         scale = const.tile([P, COLS], F32)
         mean_scaled = const.tile([P, COLS], F32)
         shift = const.tile([P, COLS], F32)
-        diagonal = const.tile([P, 2, P], F32)
-        mean_square = const.tile([P, 2], F32)
+
+        def relaid(g, h, m):
+            first = 32 * h + 4 * g + m
+            by_unit = second_turn[HALF * h : HALF * (h + 1), 0 : 2 * P].rearrange("p (u c) -> p u c", u=2)
+            return by_unit[:, :, first : first + 3 : 2]
+
+        def own_half(tile, g, h):
+            return tile[HALF * h : HALF * (h + 1), 4 * g : 4 * g + 4].rearrange("p (u e) -> p u e", u=2)
+
         for g in range(PASSES):
-            for unit in range(2 * g, 2 * g + 2):
-                if unit in VECTOR_UNITS:
-                    for e in range(2):
-                        nc.vector.bn_aggr(out=mean_var[:, 2 * unit + e, :], in_=stats[:, unit, :, 3 * e : 3 * e + 3])
-            if TENSOR_UNIT // 2 == g:
-                own = slice(2 * TENSOR_UNIT, 2 * TENSOR_UNIT + 2)
-                for e in range(2):
-                    nc.vector.scalar_tensor_tensor(
-                        out=diagonal[:, e, :], in0=grams[e][:, 0:P], scalar=1.0 / ROWS, in1=ident[:],
-                        op0=ALU.mult, op1=ALU.mult, accum_out=mean_square[:, e : e + 1],
-                    )
-                    nc.vector.tensor_scalar_mul(
-                        out=mean_var[:, 2 * TENSOR_UNIT + e, 0:1], in0=grams[e][:, P : P + 1], scalar1=1.0 / ROWS
-                    )
-                nc.vector.tensor_mul(out=square[:], in0=mean_var[:, own, 0], in1=mean_var[:, own, 0])
-                nc.vector.tensor_sub(out=mean_var[:, own, 1], in0=mean_square[:], in1=square[:])
-            if SCALAR_UNIT // 2 == g:
-                nc.vector.tensor_reduce(out=totals[:], in_=sums[:], axis=AXIS.X, op=ALU.add)
-                own = slice(2 * SCALAR_UNIT, 2 * SCALAR_UNIT + 2)
-                nc.vector.scalar_tensor_tensor(
-                    out=mean_var[:, own, 0], in0=totals[:, 0, :], scalar=-1.0 / ROWS, in1=pivot[:, 1:6:3],
-                    op0=ALU.mult, op1=ALU.add,
-                )
-                nc.vector.scalar_tensor_tensor(
-                    out=square[:], in0=totals[:, 0, :], scalar=1.0 / (ROWS * ROWS), in1=totals[:, 0, :],
-                    op0=ALU.mult, op1=ALU.mult,
-                )
-                nc.vector.scalar_tensor_tensor(
-                    out=mean_var[:, own, 1], in0=totals[:, 1, :], scalar=1.0 / ROWS, in1=square[:],
-                    op0=ALU.mult, op1=ALU.subtract,
-                )
+            for h in range(2):
+                nc.vector.tensor_scalar_add(out=own_half(var_eps, g, h), in0=relaid(g, h, 1), scalar1=BN_EPS)
             cols = slice(4 * g, 4 * g + 4)
-            nc.vector.tensor_scalar_add(out=var_eps[:, cols], in0=mean_var[:, cols, 1], scalar1=BN_EPS)
             nc.gpsimd.tensor_tensor(out=rstd[:, cols], in0=var_eps[:, cols], in1=neg_half[:, cols], op=ALU.pow)
+        for g in range(PASSES):
+            for h in range(2):
+                nc.vector.tensor_copy(out=own_half(mean, g, h), in_=relaid(g, h, 0))
         for g in range(PASSES):
             cols = slice(4 * g, 4 * g + 4)
             nc.vector.tensor_mul(out=scale[:, cols], in0=rstd[:, cols], in1=gain[:, cols])
-            nc.vector.tensor_mul(out=mean_scaled[:, cols], in0=mean_var[:, cols, 0], in1=scale[:, cols])
+            nc.vector.tensor_mul(out=mean_scaled[:, cols], in0=mean[:, cols], in1=scale[:, cols])
             nc.vector.tensor_sub(out=shift[:, cols], in0=beta[:, cols], in1=mean_scaled[:, cols])
 
         neg_max = const.tile([P, TILES], F32)

@@ -28,11 +28,12 @@ LN_GROUPS = 4
 LN_AFTER = (4, 8, 12, 14, 15, 16)
 STAT_RUN = 512
 STAT_CHUNKS = 2 * ROWS // STAT_RUN
-BLOCKS = FEATURES // (2 * P)
+VECTOR_UNITS = (0, 1)
+SCALAR_BLOCK = 0
+TENSOR_BLOCK = 1
+DIRECT_GROUPS = 2
+BLOCK_WORDS = CLASSES // 2
 HALF = P // 2
-VECTOR_BLOCKS = (0, 1)
-SCALAR_BLOCK = 2
-TENSOR_BLOCK = 3
 PAD = 8
 PITCH = CLASSES + PAD
 
@@ -47,15 +48,16 @@ def transpose_words(nc, zt_pool, ident, z_group, unit):
     return zt
 
 
-def transpose_block(nc, zt_pool, ident, z_group, b):
+def transpose_block(nc, zt_pool, ident, z_group, h):
+    first = BLOCK_WORDS + P * h
     zt = zt_pool.tile([P, GROUP_TILES, P], F32, name="zt")
     for j in range(GROUP_TILES):
-        nc.tensor.transpose(zt[:, j, :], z_group[:, j, P * b : P * (b + 1)], ident[:])
+        nc.tensor.transpose(zt[:, j, :], z_group[:, j, first : first + P], ident[:])
     return zt
 
 
 def add_products(nc, gram, z_group, j, e, start, stop):
-    first = 2 * P * TENSOR_BLOCK + e
+    first = 2 * (BLOCK_WORDS + P * TENSOR_BLOCK) + e
     values = z_group[:, j, :].bitcast(BF16)
     nc.tensor.matmul(
         out=gram[:, 0 : P + 1],
@@ -121,7 +123,7 @@ def tile_binarymlp_pb_t_kernel(tc, z2, g2, beta2, W3_words, W3_scales, b3, out):
         ident = const.tile([P, P], F32)
         make_identity(nc, ident[:])
 
-        stats = const.tile([P, len(VECTOR_BLOCKS), STAT_CHUNKS, 6], F32)
+        stats = const.tile([P, len(VECTOR_UNITS), STAT_CHUNKS, 6], F32)
         pivot = const.tile([P, 6], F32)
         sums = const.tile([P, 2, 2, GROUPS], F32)
         gain = const.tile([P, COLS], F32)
@@ -131,30 +133,40 @@ def tile_binarymlp_pb_t_kernel(tc, z2, g2, beta2, W3_words, W3_scales, b3, out):
         nc.vector.memset(moments[:], 0.0)
         turned = const.tile([P, 2, P], F32)
         nc.vector.memset(turned[:], 0.0)
+        value_sums = const.tile([P, GROUP_TILES, 2 * P], F32)
+        ones = const.tile([P, 1], F32)
+        nc.vector.memset(ones[:], 1.0)
+        nc.vector.memset(sums[:], 0.0)
+        block_values = [z_group[:, :, BLOCK_WORDS + P * SCALAR_BLOCK : BLOCK_WORDS + P * (SCALAR_BLOCK + 1)].bitcast(BF16) for z_group in z_groups]
         grams = [acc_pool.tile([P, CLASSES], F32, name="acc") for e in range(2)]
         for c in range(GROUPS):
-            for b in (SCALAR_BLOCK,) + VECTOR_BLOCKS:
-                zt = transpose_block(nc, zt_pool, ident, z_groups[c], b)
-                if b == SCALAR_BLOCK:
-                    if c == 0:
-                        nc.vector.bn_stats(out=pivot[:], in_=as_values(zt)[:, 0:STAT_RUN])
-                    for e in range(2):
-                        for power, func in enumerate((ACT.Identity, ACT.Square)):
-                            unread = scratch.tile([P, GROUP_ROWS], BF16)
-                            nc.scalar.activation(
-                                out=unread[:],
-                                in_=as_pairs(zt)[:, :, e],
-                                func=func,
-                                bias=pivot[:, 3 * e + 1 : 3 * e + 2],
-                                scale=-1.0,
-                                accum_out=sums[:, power, e, c : c + 1],
-                            )
-                else:
-                    for s in range(2):
-                        nc.vector.bn_stats(
-                            out=stats[:, b, 2 * c + s, :],
-                            in_=as_values(zt)[:, STAT_RUN * s : STAT_RUN * (s + 1)],
-                        )
+            zt = transpose_block(nc, zt_pool, ident, z_groups[c], SCALAR_BLOCK)
+            if c == 0:
+                nc.vector.bn_stats(out=pivot[:], in_=as_values(zt)[:, 0:STAT_RUN])
+            for e in range(2):
+                for power, func in ((0, ACT.Identity), (1, ACT.Square)):
+                    if power == 0 and c < GROUPS - DIRECT_GROUPS:
+                        continue
+                    unread = scratch.tile([P, GROUP_ROWS], BF16)
+                    nc.scalar.activation(
+                        out=unread[:],
+                        in_=as_pairs(zt)[:, :, e],
+                        func=func,
+                        bias=pivot[:, 3 * e + 1 : 3 * e + 2],
+                        scale=-1.0,
+                        accum_out=sums[:, power, e, c : c + 1],
+                    )
+            if 1 <= c < GROUPS - DIRECT_GROUPS:
+                nc.gpsimd.tensor_tensor(
+                    out=value_sums[:], in0=block_values[0] if c == 1 else value_sums[:], in1=block_values[c], op=ALU.add
+                )
+            for unit in VECTOR_UNITS:
+                zt = transpose_words(nc, zt_pool, ident, z_groups[c], unit)
+                for s in range(2):
+                    nc.vector.bn_stats(
+                        out=stats[:, unit, 2 * c + s, :],
+                        in_=as_values(zt)[:, STAT_RUN * s : STAT_RUN * (s + 1)],
+                    )
             for j in range(GROUP_TILES):
                 for e in range(2):
                     add_products(
@@ -166,46 +178,79 @@ def tile_binarymlp_pb_t_kernel(tc, z2, g2, beta2, W3_words, W3_scales, b3, out):
                 nc.vector.tensor_copy(out=beta[:], in_=beta_bf[:].rearrange("p g t -> p (g t)"))
                 nc.vector.tensor_copy(out=bias[:], in_=bias_bf[:])
 
+        z_sum = acc_pool.tile([P, CLASSES], F32, name="acc")
+        for e in range(2):
+            for j in range(GROUP_TILES):
+                nc.tensor.matmul(
+                    out=z_sum[:, e : e + 1], lhsT=value_sums[:, j, e : 2 * P : 2], rhs=ones[:],
+                    start=(j == 0), stop=(j == GROUP_TILES - 1),
+                )
+
         zts = {0: [transpose_words(nc, zt_pool, ident, z_groups[0], unit) for unit in range(UNITS - 1)]}
 
+        mean_var = const.tile([P, COLS, 2], F32)
+        var_eps = const.tile([P, COLS], F32)
+        rstd = const.tile([P, COLS], F32)
+        scale = const.tile([P, COLS], F32)
+        mean_scaled = const.tile([P, COLS], F32)
+        shift = const.tile([P, COLS], F32)
         totals = const.tile([P, 2, 2], F32)
-        square = const.tile([P, 2], F32)
+        deviation = const.tile([P, 2], F32)
+        square = const.tile([P, 2, 2], F32)
         diagonal = const.tile([P, 2, P], F32)
         mean_square = const.tile([P, 2], F32)
 
-        def columns(b):
-            g, h = divmod(b, 2)
-            return moments[:, 32 * h + 4 * g : 32 * h + 4 * g + 4].rearrange("p (e m) -> p e m", m=2)
+        def inverse_deviation(g):
+            cols = slice(4 * g, 4 * g + 4)
+            nc.gpsimd.tensor_tensor(out=rstd[:, cols], in0=var_eps[:, cols], in1=neg_half[:, cols], op=ALU.pow)
 
-        own = columns(TENSOR_BLOCK)
+        def scale_and_shift(g):
+            cols = slice(4 * g, 4 * g + 4)
+            nc.vector.tensor_mul(out=scale[:, cols], in0=rstd[:, cols], in1=gain[:, cols])
+            nc.vector.tensor_mul(out=mean_scaled[:, cols], in0=mean_var[:, cols, 0], in1=scale[:, cols])
+            nc.vector.tensor_sub(out=shift[:, cols], in0=beta[:, cols], in1=mean_scaled[:, cols])
+
+        for unit in VECTOR_UNITS:
+            for e in range(2):
+                nc.vector.bn_aggr(out=mean_var[:, 2 * unit + e, :], in_=stats[:, unit, :, 3 * e : 3 * e + 3])
+        nc.vector.tensor_scalar_add(out=var_eps[:, 0:4], in0=mean_var[:, 0:4, 1], scalar1=BN_EPS)
+        inverse_deviation(0)
+
+        def columns(h):
+            return moments[:, 32 * h : 32 * h + 4].rearrange("p (e m) -> p e m", m=2)
+
+        of_tensor, of_scalar = columns(TENSOR_BLOCK), columns(SCALAR_BLOCK)
+        for e in range(2):
+            nc.vector.tensor_scalar_mul(out=of_tensor[:, e, 0:1], in0=grams[e][:, P : P + 1], scalar1=1.0 / ROWS)
+        nc.vector.scalar_tensor_tensor(
+            out=deviation[:], in0=pivot[:, 1:6:3], scalar=-1.0 * (GROUPS - DIRECT_GROUPS) * GROUP_ROWS, in1=z_sum[:, 0:2],
+            op0=ALU.mult, op1=ALU.add,
+        )
+        nc.vector.tensor_reduce(out=totals[:], in_=sums[:], axis=AXIS.X, op=ALU.add)
         for e in range(2):
             nc.vector.scalar_tensor_tensor(
                 out=diagonal[:, e, :], in0=grams[e][:, 0:P], scalar=1.0 / ROWS, in1=ident[:],
                 op0=ALU.mult, op1=ALU.mult, accum_out=mean_square[:, e : e + 1],
             )
-            nc.vector.tensor_scalar_mul(out=own[:, e, 0:1], in0=grams[e][:, P : P + 1], scalar1=1.0 / ROWS)
-        nc.vector.tensor_mul(out=square[:], in0=own[:, :, 0], in1=own[:, :, 0])
-        for b in VECTOR_BLOCKS:
-            for e in range(2):
-                nc.vector.bn_aggr(out=columns(b)[:, e, :], in_=stats[:, b, :, 3 * e : 3 * e + 3])
-        nc.vector.tensor_sub(out=own[:, :, 1], in0=mean_square[:], in1=square[:])
-        nc.vector.tensor_reduce(out=totals[:], in_=sums[:], axis=AXIS.X, op=ALU.add)
-        own = columns(SCALAR_BLOCK)
+        nc.vector.tensor_sub(out=deviation[:], in0=deviation[:], in1=totals[:, 0, :])
+        nc.vector.tensor_mul(out=square[:, TENSOR_BLOCK, :], in0=of_tensor[:, :, 0], in1=of_tensor[:, :, 0])
         nc.vector.scalar_tensor_tensor(
-            out=own[:, :, 0], in0=totals[:, 0, :], scalar=-1.0 / ROWS, in1=pivot[:, 1:6:3],
-            op0=ALU.mult, op1=ALU.add,
-        )
-        nc.vector.scalar_tensor_tensor(
-            out=square[:], in0=totals[:, 0, :], scalar=1.0 / (ROWS * ROWS), in1=totals[:, 0, :],
+            out=square[:, SCALAR_BLOCK, :], in0=deviation[:], scalar=1.0 / (ROWS * ROWS), in1=deviation[:],
             op0=ALU.mult, op1=ALU.mult,
         )
         nc.vector.scalar_tensor_tensor(
-            out=own[:, :, 1], in0=totals[:, 1, :], scalar=1.0 / ROWS, in1=square[:],
+            out=of_scalar[:, :, 0], in0=deviation[:], scalar=1.0 / ROWS, in1=pivot[:, 1:6:3],
+            op0=ALU.mult, op1=ALU.add,
+        )
+        nc.vector.tensor_sub(out=of_tensor[:, :, 1], in0=mean_square[:], in1=square[:, TENSOR_BLOCK, :])
+        nc.vector.scalar_tensor_tensor(
+            out=of_scalar[:, :, 1], in0=totals[:, 1, :], scalar=1.0 / ROWS, in1=square[:, SCALAR_BLOCK, :],
             op0=ALU.mult, op1=ALU.subtract,
         )
 
         first_turn = acc_pool.tile([P, CLASSES], F32, name="acc")
         nc.tensor.transpose(first_turn[:, 0:P], moments[:], ident[:])
+        scale_and_shift(0)
         nc.vector.tensor_copy(
             out=turned[0:HALF, :, :], in_=first_turn[0:HALF, 0:P].unsqueeze(1).to_broadcast([HALF, 2, P])
         )
@@ -216,34 +261,20 @@ def tile_binarymlp_pb_t_kernel(tc, z2, g2, beta2, W3_words, W3_scales, b3, out):
             )
         zts[0].append(transpose_words(nc, zt_pool, ident, z_groups[0], UNITS - 1))
 
-        mean = const.tile([P, COLS], F32)
-        var_eps = const.tile([P, COLS], F32)
-        rstd = const.tile([P, COLS], F32)
-        scale = const.tile([P, COLS], F32)
-        mean_scaled = const.tile([P, COLS], F32)
-        shift = const.tile([P, COLS], F32)
-
-        def relaid(g, h, m):
-            first = 32 * h + 4 * g + m
+        def relaid(h, m):
+            first = 32 * h + m
             by_unit = second_turn[HALF * h : HALF * (h + 1), 0 : 2 * P].rearrange("p (u c) -> p u c", u=2)
             return by_unit[:, :, first : first + 3 : 2]
 
-        def own_half(tile, g, h):
-            return tile[HALF * h : HALF * (h + 1), 4 * g : 4 * g + 4].rearrange("p (u e) -> p u e", u=2)
+        def second_pass(tile_columns, h):
+            return tile_columns[HALF * h : HALF * (h + 1)].rearrange("p (u e) -> p u e", u=2)
 
-        for g in range(PASSES):
-            for h in range(2):
-                nc.vector.tensor_scalar_add(out=own_half(var_eps, g, h), in0=relaid(g, h, 1), scalar1=BN_EPS)
-            cols = slice(4 * g, 4 * g + 4)
-            nc.gpsimd.tensor_tensor(out=rstd[:, cols], in0=var_eps[:, cols], in1=neg_half[:, cols], op=ALU.pow)
-        for g in range(PASSES):
-            for h in range(2):
-                nc.vector.tensor_copy(out=own_half(mean, g, h), in_=relaid(g, h, 0))
-        for g in range(PASSES):
-            cols = slice(4 * g, 4 * g + 4)
-            nc.vector.tensor_mul(out=scale[:, cols], in0=rstd[:, cols], in1=gain[:, cols])
-            nc.vector.tensor_mul(out=mean_scaled[:, cols], in0=mean[:, cols], in1=scale[:, cols])
-            nc.vector.tensor_sub(out=shift[:, cols], in0=beta[:, cols], in1=mean_scaled[:, cols])
+        for h in range(2):
+            nc.vector.tensor_scalar_add(out=second_pass(var_eps[:, 4:8], h), in0=relaid(h, 1), scalar1=BN_EPS)
+        inverse_deviation(1)
+        for h in range(2):
+            nc.vector.tensor_copy(out=second_pass(mean_var[:, 4:8, 0], h), in_=relaid(h, 0))
+        scale_and_shift(1)
 
         neg_max = const.tile([P, TILES], F32)
         sum_exp = const.tile([P, TILES], F32)

@@ -34,8 +34,6 @@ TENSOR_BLOCK = 1
 DIRECT_GROUPS = 2
 BLOCK_WORDS = CLASSES // 2
 HALF = P // 2
-PAD = 8
-PITCH = CLASSES + PAD
 
 FLOPS = 2 * ROWS * FEATURES * CLASSES
 
@@ -56,16 +54,9 @@ def transpose_block(nc, zt_pool, ident, z_group, h):
     return zt
 
 
-def add_products(nc, gram, z_group, j, e, start, stop):
+def tensor_block(z_group, j, e):
     first = 2 * (BLOCK_WORDS + P * TENSOR_BLOCK) + e
-    values = z_group[:, j, :].bitcast(BF16)
-    nc.tensor.matmul(
-        out=gram[:, 0 : P + 1],
-        lhsT=values[:, first : first + 2 * P : 2],
-        rhs=values[:, first : first + 2 * P + 1 : 2],
-        start=start,
-        stop=stop,
-    )
+    return z_group[:, j, :].bitcast(BF16)[:, first : first + 2 * P - 1 : 2]
 
 
 def as_values(zt):
@@ -92,10 +83,9 @@ def tile_binarymlp_pb_t_kernel(tc, z2, g2, beta2, W3_words, W3_scales, b3, out):
 
         z_groups = []
         for c in range(GROUPS):
-            z_group = resident.tile([P, GROUP_TILES, PITCH], F32, name="z_group%d" % c)
-            nc.vector.memset(z_group[:, :, CLASSES : CLASSES + 8].bitcast(BF16), 1.0)
+            z_group = resident.tile([P, GROUP_TILES, CLASSES], F32, name="z_group%d" % c)
             nc.sync.dma_start(
-                out=z_group[:, :, 0:CLASSES].bitcast(BF16),
+                out=z_group[:].bitcast(BF16),
                 in_=z_rows[:, GROUP_TILES * c : GROUP_TILES * (c + 1), :],
             )
             z_groups.append(z_group)
@@ -136,9 +126,12 @@ def tile_binarymlp_pb_t_kernel(tc, z2, g2, beta2, W3_words, W3_scales, b3, out):
         value_sums = const.tile([P, GROUP_TILES, 2 * P], F32)
         ones = const.tile([P, 1], F32)
         nc.vector.memset(ones[:], 1.0)
+        ones_bf = const.tile([P, 1], BF16)
+        nc.vector.memset(ones_bf[:], 1.0)
         nc.vector.memset(sums[:], 0.0)
         block_values = [z_group[:, :, BLOCK_WORDS + P * SCALAR_BLOCK : BLOCK_WORDS + P * (SCALAR_BLOCK + 1)].bitcast(BF16) for z_group in z_groups]
         grams = [acc_pool.tile([P, CLASSES], F32, name="acc") for e in range(2)]
+        plain_sums = acc_pool.tile([P, CLASSES], F32, name="acc")
         for c in range(GROUPS):
             zt = transpose_block(nc, zt_pool, ident, z_groups[c], SCALAR_BLOCK)
             if c == 0:
@@ -169,16 +162,23 @@ def tile_binarymlp_pb_t_kernel(tc, z2, g2, beta2, W3_words, W3_scales, b3, out):
                     )
             for j in range(GROUP_TILES):
                 for e in range(2):
-                    add_products(
-                        nc, grams[e], z_groups[c], j, e,
+                    block = tensor_block(z_groups[c], j, e)
+                    nc.tensor.matmul(
+                        out=grams[e][:, 0:P], lhsT=block, rhs=block,
                         start=(c == 0 and j == 0), stop=(c == GROUPS - 1 and j == GROUP_TILES - 1),
+                    )
+            for e in range(2):
+                for j in range(GROUP_TILES):
+                    nc.tensor.matmul(
+                        out=plain_sums[:, GROUPS * e + c : GROUPS * e + c + 1], lhsT=tensor_block(z_groups[c], j, e), rhs=ones_bf[:],
+                        start=(j == 0), stop=(j == GROUP_TILES - 1),
                     )
             if c == 0:
                 nc.vector.tensor_copy(out=gain[:], in_=gain_bf[:].rearrange("p g t -> p (g t)"))
                 nc.vector.tensor_copy(out=beta[:], in_=beta_bf[:].rearrange("p g t -> p (g t)"))
                 nc.vector.tensor_copy(out=bias[:], in_=bias_bf[:])
 
-        z_sum = acc_pool.tile([P, CLASSES], F32, name="acc")
+        z_sum = plain_sums[:, 2 * GROUPS : 2 * GROUPS + 2]
         for e in range(2):
             for j in range(GROUP_TILES):
                 nc.tensor.matmul(
@@ -198,6 +198,7 @@ def tile_binarymlp_pb_t_kernel(tc, z2, g2, beta2, W3_words, W3_scales, b3, out):
         deviation = const.tile([P, 2], F32)
         square = const.tile([P, 2, 2], F32)
         diagonal = const.tile([P, 2, P], F32)
+        tensor_sums = const.tile([P, 2], F32)
         mean_square = const.tile([P, 2], F32)
 
         def inverse_deviation(g):
@@ -220,10 +221,11 @@ def tile_binarymlp_pb_t_kernel(tc, z2, g2, beta2, W3_words, W3_scales, b3, out):
             return moments[:, 32 * h : 32 * h + 4].rearrange("p (e m) -> p e m", m=2)
 
         of_tensor, of_scalar = columns(TENSOR_BLOCK), columns(SCALAR_BLOCK)
-        for e in range(2):
-            nc.vector.tensor_scalar_mul(out=of_tensor[:, e, 0:1], in0=grams[e][:, P : P + 1], scalar1=1.0 / ROWS)
+        nc.vector.tensor_reduce(
+            out=tensor_sums[:], in_=plain_sums[:, 0 : 2 * GROUPS].rearrange("p (e c) -> p e c", e=2), axis=AXIS.X, op=ALU.add
+        )
         nc.vector.scalar_tensor_tensor(
-            out=deviation[:], in0=pivot[:, 1:6:3], scalar=-1.0 * (GROUPS - DIRECT_GROUPS) * GROUP_ROWS, in1=z_sum[:, 0:2],
+            out=deviation[:], in0=pivot[:, 1:6:3], scalar=-1.0 * (GROUPS - DIRECT_GROUPS) * GROUP_ROWS, in1=z_sum,
             op0=ALU.mult, op1=ALU.add,
         )
         nc.vector.tensor_reduce(out=totals[:], in_=sums[:], axis=AXIS.X, op=ALU.add)
@@ -232,6 +234,7 @@ def tile_binarymlp_pb_t_kernel(tc, z2, g2, beta2, W3_words, W3_scales, b3, out):
                 out=diagonal[:, e, :], in0=grams[e][:, 0:P], scalar=1.0 / ROWS, in1=ident[:],
                 op0=ALU.mult, op1=ALU.mult, accum_out=mean_square[:, e : e + 1],
             )
+        nc.vector.tensor_scalar_mul(out=of_tensor[:, :, 0], in0=tensor_sums[:], scalar1=1.0 / ROWS)
         nc.vector.tensor_sub(out=deviation[:], in0=deviation[:], in1=totals[:, 0, :])
         nc.vector.tensor_mul(out=square[:, TENSOR_BLOCK, :], in0=of_tensor[:, :, 0], in1=of_tensor[:, :, 0])
         nc.vector.scalar_tensor_tensor(
@@ -335,12 +338,12 @@ def tile_binarymlp_pb_t_kernel(tc, z2, g2, beta2, W3_words, W3_scales, b3, out):
         def logits_and_max(c, accs):
             for j in range(GROUP_TILES + 1):
                 if j < GROUP_TILES:
-                    nc.vector.tensor_tensor(out=z_groups[c][:, j, 0:CLASSES], in0=accs[j][:], in1=bias[:], op=ALU.add)
+                    nc.vector.tensor_tensor(out=z_groups[c][:, j, :], in0=accs[j][:], in1=bias[:], op=ALU.add)
                 if j >= 1:
                     col = GROUP_TILES * c + j - 1
                     nc.vector.tensor_reduce(
                         out=neg_max[:, col : col + 1],
-                        in_=z_groups[c][:, j - 1, 0:CLASSES],
+                        in_=z_groups[c][:, j - 1, :],
                         axis=AXIS.X,
                         op=ALU.max,
                         negate=True,
@@ -352,7 +355,7 @@ def tile_binarymlp_pb_t_kernel(tc, z2, g2, beta2, W3_words, W3_scales, b3, out):
                 unread = scratch.tile([P, CLASSES], BF16)
                 nc.scalar.activation(
                     out=unread[:],
-                    in_=z_groups[c][:, j, 0:CLASSES],
+                    in_=z_groups[c][:, j, :],
                     func=ACT.Exp,
                     bias=neg_max[:, col : col + 1],
                     scale=1.0,
@@ -371,14 +374,14 @@ def tile_binarymlp_pb_t_kernel(tc, z2, g2, beta2, W3_words, W3_scales, b3, out):
                 for j in range(GROUP_TILES):
                     col = GROUP_TILES * (c - c_first) + j
                     engine.tensor_scalar(
-                        out=z_groups[c][:, j, 0:CLASSES],
-                        in0=z_groups[c][:, j, 0:CLASSES],
+                        out=z_groups[c][:, j, :],
+                        in0=z_groups[c][:, j, :],
                         scalar1=1.0,
                         scalar2=neg_shift[:, col : col + 1],
                         op0=ALU.mult,
                         op1=ALU.add,
                     )
-                nc.sync.dma_start(out=out_rows[:, GROUP_TILES * c : GROUP_TILES * (c + 1), :], in_=z_groups[c][:, :, 0:CLASSES])
+                nc.sync.dma_start(out=out_rows[:, GROUP_TILES * c : GROUP_TILES * (c + 1), :], in_=z_groups[c][:])
 
         accs_of, grouped_of = {}, {}
         finished = 0

@@ -90,6 +90,13 @@ def tile_binarymlp_pb_t_kernel(tc, z2, g2, beta2, W3_words, W3_scales, b3, out):
             )
             z_groups.append(z_group)
 
+        gain = const.tile([P, PASSES, 4], BF16)
+        beta = const.tile([P, PASSES, 4], BF16)
+        bias = const.tile([P, CLASSES], BF16)
+        with nc.allow_non_contiguous_dma(reason="four neighbouring features to a partition"):
+            nc.sync.dma_start(out=gain[:], in_=g2.rearrange("(g p t) -> p g t", g=PASSES, t=4))
+            nc.sync.dma_start(out=beta[:], in_=beta2.rearrange("(g p t) -> p g t", g=PASSES, t=4))
+        nc.sync.dma_start(out=bias[:], in_=b3.partition_broadcast(P))
         w_scales = const.tile([P, PASSES, CLASSES], U8, align_bytes=64)
         nc.vector.memset(w_scales[:].bitcast(I32), 0)
         w_words = const.tile([P, PASSES, 2 * CLASSES], U8, align_bytes=64)
@@ -101,13 +108,6 @@ def tile_binarymlp_pb_t_kernel(tc, z2, g2, beta2, W3_words, W3_scales, b3, out):
                 in_=W3_scales.bitcast(I32)[:, 4 * q : 4 * q + 4, :].rearrange("g r n -> r g n"),
             )
 
-        gain_bf = const.tile([P, PASSES, 4], BF16)
-        beta_bf = const.tile([P, PASSES, 4], BF16)
-        bias_bf = const.tile([P, CLASSES], BF16)
-        with nc.allow_non_contiguous_dma(reason="four neighbouring features to a partition"):
-            nc.scalar.dma_start(out=gain_bf[:], in_=g2.rearrange("(g p t) -> p g t", g=PASSES, t=4))
-            nc.scalar.dma_start(out=beta_bf[:], in_=beta2.rearrange("(g p t) -> p g t", g=PASSES, t=4))
-        nc.scalar.dma_start(out=bias_bf[:], in_=b3.partition_broadcast(P))
         neg_half = const.tile([P, COLS], F32)
         nc.vector.memset(neg_half[:], -0.5)
         ident = const.tile([P, P], F32)
@@ -116,9 +116,6 @@ def tile_binarymlp_pb_t_kernel(tc, z2, g2, beta2, W3_words, W3_scales, b3, out):
         stats = const.tile([P, len(VECTOR_UNITS), STAT_CHUNKS, 6], F32)
         pivot = const.tile([P, 6], F32)
         sums = const.tile([P, 2, 2, GROUPS], F32)
-        gain = const.tile([P, COLS], F32)
-        beta = const.tile([P, COLS], F32)
-        bias = const.tile([P, CLASSES], F32)
         moments = const.tile([P, P], F32)
         nc.vector.memset(moments[:], 0.0)
         turned = const.tile([P, 2, P], F32)
@@ -173,10 +170,6 @@ def tile_binarymlp_pb_t_kernel(tc, z2, g2, beta2, W3_words, W3_scales, b3, out):
                         out=plain_sums[:, GROUPS * e + c : GROUPS * e + c + 1], lhsT=tensor_block(z_groups[c], j, e), rhs=ones_bf[:],
                         start=(j == 0), stop=(j == GROUP_TILES - 1),
                     )
-            if c == 0:
-                nc.vector.tensor_copy(out=gain[:], in_=gain_bf[:].rearrange("p g t -> p (g t)"))
-                nc.vector.tensor_copy(out=beta[:], in_=beta_bf[:].rearrange("p g t -> p (g t)"))
-                nc.vector.tensor_copy(out=bias[:], in_=bias_bf[:])
 
         z_sum = plain_sums[:, 2 * GROUPS : 2 * GROUPS + 2]
         for e in range(2):
@@ -207,9 +200,9 @@ def tile_binarymlp_pb_t_kernel(tc, z2, g2, beta2, W3_words, W3_scales, b3, out):
 
         def scale_and_shift(g):
             cols = slice(4 * g, 4 * g + 4)
-            nc.vector.tensor_mul(out=scale[:, cols], in0=rstd[:, cols], in1=gain[:, cols])
+            nc.vector.tensor_mul(out=scale[:, cols], in0=rstd[:, cols], in1=gain[:, g, :])
             nc.vector.tensor_mul(out=mean_scaled[:, cols], in0=mean_var[:, cols, 0], in1=scale[:, cols])
-            nc.vector.tensor_sub(out=shift[:, cols], in0=beta[:, cols], in1=mean_scaled[:, cols])
+            nc.vector.tensor_sub(out=shift[:, cols], in0=beta[:, g, :], in1=mean_scaled[:, cols])
 
         for unit in VECTOR_UNITS:
             for e in range(2):

@@ -24,8 +24,9 @@ TILES = ROWS // P
 GROUP_TILES = 4
 GROUPS = TILES // GROUP_TILES
 GROUP_ROWS = GROUP_TILES * P
-LN_GROUPS = 4
-LN_AFTER = (4, 8, 12, 14, 15, 16)
+LN_GROUPS = 5
+LN_AFTER = (5, 10, 14, 16)
+LATE_GROUP = 13
 STAT_RUN = 512
 STAT_CHUNKS = 2 * ROWS // STAT_RUN
 VECTOR_UNITS = (0, 1)
@@ -362,21 +363,19 @@ def tile_binarymlp_pb_t_kernel(tc, z2, g2, beta2, W3_words, W3_scales, b3, out):
             engine.tensor_tensor(out=neg_shift[:, 0 : hi - lo], in0=neg_max[:, lo:hi], in1=log_sum[:, lo:hi], op=ALU.subtract)
             return neg_shift
 
-        def subtract_and_store(neg_shift, c_first, c_from, c_to, engine):
-            for c in range(c_from, c_to):
-                for j in range(GROUP_TILES):
-                    col = GROUP_TILES * (c - c_first) + j
-                    engine.tensor_scalar(
-                        out=z_groups[c][:, j, :],
-                        in0=z_groups[c][:, j, :],
-                        scalar1=1.0,
-                        scalar2=neg_shift[:, col : col + 1],
-                        op0=ALU.mult,
-                        op1=ALU.add,
-                    )
-                nc.sync.dma_start(out=out_rows[:, GROUP_TILES * c : GROUP_TILES * (c + 1), :], in_=z_groups[c][:])
+        def subtract_and_store(neg_shift, c_first, c, tiles, engine=None):
+            for j in tiles:
+                col = GROUP_TILES * (c - c_first) + j
+                values, shift_of_rows = z_groups[c][:, j, :], neg_shift[:, col : col + 1]
+                if engine is None:
+                    nc.scalar.activation(out=values, in_=values, func=ACT.Identity, bias=shift_of_rows, scale=1.0)
+                else:
+                    engine.tensor_scalar(out=values, in0=values, scalar1=1.0, scalar2=shift_of_rows, op0=ALU.mult, op1=ALU.add)
+            first = GROUP_TILES * c + tiles[0]
+            nc.sync.dma_start(out=out_rows[:, first : first + len(tiles), :], in_=z_groups[c][:, tiles[0] : tiles[0] + len(tiles), :])
 
         accs_of, grouped_of = {}, {}
+        all_tiles = list(range(GROUP_TILES))
         finished = 0
         for k in range(GROUPS + 2):
             if k == GROUPS:
@@ -395,7 +394,19 @@ def tile_binarymlp_pb_t_kernel(tc, z2, g2, beta2, W3_words, W3_scales, b3, out):
                 accs_of[k - 1] = classify(k - 1, acc_pool, "acc")
             if k < GROUPS:
                 grouped_of[k] = regroup(k)
-            if k - 1 in LN_AFTER:
-                engine = nc.vector if k - 1 == GROUPS else nc.gpsimd
-                subtract_and_store(shifts(finished, k - 1, engine), finished, finished, k - 1, engine)
+            if k == GROUPS + 1:
+                subtract_and_store(late_shift, late_first, LATE_GROUP, all_tiles, nc.vector)
+            if k - 1 in LN_AFTER and k - 1 < GROUPS:
+                neg_shift = shifts(finished, k - 1, nc.gpsimd)
+                for c in range(finished, k - 1):
+                    if c == LATE_GROUP:
+                        late_shift, late_first = neg_shift, finished
+                    else:
+                        subtract_and_store(neg_shift, finished, c, all_tiles, nc.gpsimd)
                 finished = k - 1
+        neg_shift = shifts(finished, GROUPS, nc.vector)
+        halves = (all_tiles[: GROUP_TILES // 2], all_tiles[GROUP_TILES // 2 :])
+        for c in range(finished, GROUPS):
+            for i, tiles in enumerate(halves):
+                engine = None if c == finished and i == 1 else nc.vector
+                subtract_and_store(neg_shift, finished, c, tiles, engine)

from contextlib import ExitStack

import concourse.mybir as mybir
from concourse.masks import make_identity

F32 = mybir.dt.float32
BF16 = mybir.dt.bfloat16
I32 = mybir.dt.int32
U8 = mybir.dt.uint8
U32 = mybir.dt.uint32
FP8X4 = mybir.dt.float8_e4m3fn_x4
FP4X4 = mybir.dt.float4_e2m1fn_x4
ALU = mybir.AluOpType
ACT = mybir.ActivationFunctionType
AXIS = mybir.AxisListType

P = 128
ROWS, FEATURES, CLASSES = 8192, 1024, 512
BN_EPS = 1e-5
PASSES = FEATURES // (4 * P)
UNITS = 2 * PASSES
COLS = 4 * PASSES
TILES = ROWS // P
GROUP_TILES = 4
GROUPS = TILES // GROUP_TILES
GROUP_ROWS = GROUP_TILES * P
LN_GROUPS = 5
LN_AFTER = (5, 10, 14, 16)
LATE_GROUP = 13
STAT_RUN = 512
STAT_CHUNKS = 2 * ROWS // STAT_RUN
VECTOR_UNITS = (0, 1)
SCALAR_BLOCK = 0
TENSOR_BLOCK = 1
DIRECT_GROUPS = 2
BLOCK_WORDS = CLASSES // 2
HALF = P // 2

FLOPS = 2 * ROWS * FEATURES * CLASSES


def transpose_words(nc, zt_pool, ident, z_group, unit):
    g, u = divmod(unit, 2)
    zt = zt_pool.tile([P, GROUP_TILES, P], F32, name="zt")
    for j in range(GROUP_TILES):
        nc.tensor.transpose(zt[:, j, :], z_group[:, j, 256 * g + u : 256 * (g + 1) : 2], ident[:])
    return zt


def transpose_block(nc, zt_pool, ident, z_group, h):
    first = BLOCK_WORDS + P * h
    zt = zt_pool.tile([P, GROUP_TILES, P], F32, name="zt")
    for j in range(GROUP_TILES):
        nc.tensor.transpose(zt[:, j, :], z_group[:, j, first : first + P], ident[:])
    return zt


def tensor_block(z_group, j, e):
    first = 2 * (BLOCK_WORDS + P * TENSOR_BLOCK) + e
    return z_group[:, j, :].bitcast(BF16)[:, first : first + 2 * P - 1 : 2]


def as_values(zt):
    return zt[:].rearrange("p j r -> p (j r)").bitcast(BF16)


def as_pairs(zt):
    return as_values(zt).rearrange("p (r e) -> p r e", e=2)


def tile_binarymlp_pb_t_kernel(tc, z2, g2, beta2, W3_words, W3_scales, b3, out):
    nc = tc.nc
    z_rows = z2.rearrange("(p j) k -> p j k", j=TILES)
    out_rows = out.rearrange("(p j) n -> p j n", j=TILES)

    with ExitStack() as ctx:
        const = ctx.enter_context(tc.tile_pool(name="const", bufs=1))
        resident = ctx.enter_context(tc.tile_pool(name="resident", bufs=1))
        work = ctx.enter_context(tc.tile_pool(name="work", bufs=2))
        scratch = ctx.enter_context(tc.tile_pool(name="scratch", bufs=4))
        zt_pool = ctx.enter_context(tc.psum_pool(name="zt_pool", bufs=UNITS))
        acc_pool = ctx.enter_context(tc.psum_pool(name="acc_pool", bufs=GROUP_TILES))
        ctx.enter_context(tc.manual_schedule())

        z_groups = []
        for c in range(GROUPS):
            z_group = resident.tile([P, GROUP_TILES, CLASSES], F32, name="z_group%d" % c)
            nc.sync.dma_start(
                out=z_group[:].bitcast(BF16),
                in_=z_rows[:, GROUP_TILES * c : GROUP_TILES * (c + 1), :],
            )
            z_groups.append(z_group)

        gain = const.tile([P, PASSES, 4], BF16)
        beta = const.tile([P, PASSES, 4], BF16)
        bias = const.tile([P, CLASSES], BF16)
        with nc.allow_non_contiguous_dma(reason="four neighbouring features to a partition"):
            nc.sync.dma_start(out=gain[:], in_=g2.rearrange("(g p t) -> p g t", g=PASSES, t=4))
            nc.sync.dma_start(out=beta[:], in_=beta2.rearrange("(g p t) -> p g t", g=PASSES, t=4))
        nc.sync.dma_start(out=bias[:], in_=b3.partition_broadcast(P))
        w_scales = const.tile([P, PASSES, CLASSES], U8, align_bytes=64)
        nc.vector.memset(w_scales[:].bitcast(I32), 0)
        w_words = const.tile([P, PASSES, 2 * CLASSES], U8, align_bytes=64)
        for g in range(PASSES):
            nc.sync.dma_start(out=w_words[:, g, :].bitcast(I32), in_=W3_words[g].bitcast(I32))
        for q in range(4):
            nc.sync.dma_start(
                out=w_scales[32 * q : 32 * q + 4, :, :].bitcast(I32),
                in_=W3_scales.bitcast(I32)[:, 4 * q : 4 * q + 4, :].rearrange("g r n -> r g n"),
            )

        neg_half = const.tile([P, COLS], F32)
        nc.vector.memset(neg_half[:], -0.5)
        ident = const.tile([P, P], F32)
        make_identity(nc, ident[:])

        stats = const.tile([P, len(VECTOR_UNITS), STAT_CHUNKS, 6], F32)
        pivot = const.tile([P, 6], F32)
        sums = const.tile([P, 2, 2, GROUPS], F32)
        moments = const.tile([P, P], F32)
        nc.vector.memset(moments[:], 0.0)
        turned = const.tile([P, 2, P], F32)
        nc.vector.memset(turned[:], 0.0)
        value_sums = const.tile([P, GROUP_TILES, 2 * P], F32)
        ones = const.tile([P, 1], F32)
        nc.vector.memset(ones[:], 1.0)
        ones_bf = const.tile([P, 1], BF16)
        nc.vector.memset(ones_bf[:], 1.0)
        nc.vector.memset(sums[:], 0.0)
        block_values = [z_group[:, :, BLOCK_WORDS + P * SCALAR_BLOCK : BLOCK_WORDS + P * (SCALAR_BLOCK + 1)].bitcast(BF16) for z_group in z_groups]
        grams = [acc_pool.tile([P, CLASSES], F32, name="acc") for e in range(2)]
        plain_sums = acc_pool.tile([P, CLASSES], F32, name="acc")
        for c in range(GROUPS):
            zt = transpose_block(nc, zt_pool, ident, z_groups[c], SCALAR_BLOCK)
            if c == 0:
                nc.vector.bn_stats(out=pivot[:], in_=as_values(zt)[:, 0:STAT_RUN])
            for e in range(2):
                for power, func in ((0, ACT.Identity), (1, ACT.Square)):
                    if power == 0 and c < GROUPS - DIRECT_GROUPS:
                        continue
                    unread = scratch.tile([P, GROUP_ROWS], BF16)
                    nc.scalar.activation(
                        out=unread[:],
                        in_=as_pairs(zt)[:, :, e],
                        func=func,
                        bias=pivot[:, 3 * e + 1 : 3 * e + 2],
                        scale=-1.0,
                        accum_out=sums[:, power, e, c : c + 1],
                    )
            if 1 <= c < GROUPS - DIRECT_GROUPS:
                nc.gpsimd.tensor_tensor(
                    out=value_sums[:], in0=block_values[0] if c == 1 else value_sums[:], in1=block_values[c], op=ALU.add
                )
            for unit in VECTOR_UNITS:
                zt = transpose_words(nc, zt_pool, ident, z_groups[c], unit)
                for s in range(2):
                    nc.vector.bn_stats(
                        out=stats[:, unit, 2 * c + s, :],
                        in_=as_values(zt)[:, STAT_RUN * s : STAT_RUN * (s + 1)],
                    )
            for j in range(GROUP_TILES):
                for e in range(2):
                    block = tensor_block(z_groups[c], j, e)
                    nc.tensor.matmul(
                        out=grams[e][:, 0:P], lhsT=block, rhs=block,
                        start=(c == 0 and j == 0), stop=(c == GROUPS - 1 and j == GROUP_TILES - 1),
                    )
            for e in range(2):
                for j in range(GROUP_TILES):
                    nc.tensor.matmul(
                        out=plain_sums[:, GROUPS * e + c : GROUPS * e + c + 1], lhsT=tensor_block(z_groups[c], j, e), rhs=ones_bf[:],
                        start=(j == 0), stop=(j == GROUP_TILES - 1),
                    )

        z_sum = plain_sums[:, 2 * GROUPS : 2 * GROUPS + 2]
        for e in range(2):
            for j in range(GROUP_TILES):
                nc.tensor.matmul(
                    out=z_sum[:, e : e + 1], lhsT=value_sums[:, j, e : 2 * P : 2], rhs=ones[:],
                    start=(j == 0), stop=(j == GROUP_TILES - 1),
                )

        zts = {0: [transpose_words(nc, zt_pool, ident, z_groups[0], unit) for unit in range(UNITS - 1)]}

        mean_var = const.tile([P, COLS, 2], F32)
        var_eps = const.tile([P, COLS], F32)
        rstd = const.tile([P, COLS], F32)
        scale = const.tile([P, COLS], F32)
        mean_scaled = const.tile([P, COLS], F32)
        shift = const.tile([P, COLS], F32)
        totals = const.tile([P, 2, 2], F32)
        deviation = const.tile([P, 2], F32)
        square = const.tile([P, 2, 2], F32)
        diagonal = const.tile([P, 2, P], F32)
        tensor_sums = const.tile([P, 2], F32)
        mean_square = const.tile([P, 2], F32)

        def inverse_deviation(g):
            cols = slice(4 * g, 4 * g + 4)
            nc.gpsimd.tensor_tensor(out=rstd[:, cols], in0=var_eps[:, cols], in1=neg_half[:, cols], op=ALU.pow)

        def scale_and_shift(g):
            cols = slice(4 * g, 4 * g + 4)
            nc.vector.tensor_mul(out=scale[:, cols], in0=rstd[:, cols], in1=gain[:, g, :])
            nc.vector.tensor_mul(out=mean_scaled[:, cols], in0=mean_var[:, cols, 0], in1=scale[:, cols])
            nc.vector.tensor_sub(out=shift[:, cols], in0=beta[:, g, :], in1=mean_scaled[:, cols])

        for unit in VECTOR_UNITS:
            for e in range(2):
                nc.vector.bn_aggr(out=mean_var[:, 2 * unit + e, :], in_=stats[:, unit, :, 3 * e : 3 * e + 3])
        nc.vector.tensor_scalar_add(out=var_eps[:, 0:4], in0=mean_var[:, 0:4, 1], scalar1=BN_EPS)
        inverse_deviation(0)

        def columns(h):
            return moments[:, 32 * h : 32 * h + 4].rearrange("p (e m) -> p e m", m=2)

        of_tensor, of_scalar = columns(TENSOR_BLOCK), columns(SCALAR_BLOCK)
        nc.vector.tensor_reduce(
            out=tensor_sums[:], in_=plain_sums[:, 0 : 2 * GROUPS].rearrange("p (e c) -> p e c", e=2), axis=AXIS.X, op=ALU.add
        )
        nc.vector.scalar_tensor_tensor(
            out=deviation[:], in0=pivot[:, 1:6:3], scalar=-1.0 * (GROUPS - DIRECT_GROUPS) * GROUP_ROWS, in1=z_sum,
            op0=ALU.mult, op1=ALU.add,
        )
        nc.vector.tensor_reduce(out=totals[:], in_=sums[:], axis=AXIS.X, op=ALU.add)
        for e in range(2):
            nc.vector.scalar_tensor_tensor(
                out=diagonal[:, e, :], in0=grams[e][:, 0:P], scalar=1.0 / ROWS, in1=ident[:],
                op0=ALU.mult, op1=ALU.mult, accum_out=mean_square[:, e : e + 1],
            )
        nc.vector.tensor_scalar_mul(out=of_tensor[:, :, 0], in0=tensor_sums[:], scalar1=1.0 / ROWS)
        nc.vector.tensor_sub(out=deviation[:], in0=deviation[:], in1=totals[:, 0, :])
        nc.vector.tensor_mul(out=square[:, TENSOR_BLOCK, :], in0=of_tensor[:, :, 0], in1=of_tensor[:, :, 0])
        nc.vector.scalar_tensor_tensor(
            out=square[:, SCALAR_BLOCK, :], in0=deviation[:], scalar=1.0 / (ROWS * ROWS), in1=deviation[:],
            op0=ALU.mult, op1=ALU.mult,
        )
        nc.vector.scalar_tensor_tensor(
            out=of_scalar[:, :, 0], in0=deviation[:], scalar=1.0 / ROWS, in1=pivot[:, 1:6:3],
            op0=ALU.mult, op1=ALU.add,
        )
        nc.vector.tensor_sub(out=of_tensor[:, :, 1], in0=mean_square[:], in1=square[:, TENSOR_BLOCK, :])
        nc.vector.scalar_tensor_tensor(
            out=of_scalar[:, :, 1], in0=totals[:, 1, :], scalar=1.0 / ROWS, in1=square[:, SCALAR_BLOCK, :],
            op0=ALU.mult, op1=ALU.subtract,
        )

        first_turn = acc_pool.tile([P, CLASSES], F32, name="acc")
        nc.tensor.transpose(first_turn[:, 0:P], moments[:], ident[:])
        scale_and_shift(0)
        nc.vector.tensor_copy(
            out=turned[0:HALF, :, :], in_=first_turn[0:HALF, 0:P].unsqueeze(1).to_broadcast([HALF, 2, P])
        )
        second_turn = acc_pool.tile([P, CLASSES], F32, name="acc")
        for u in range(2):
            nc.tensor.transpose(
                second_turn[:, P * u : P * (u + 1)], turned[:].rearrange("p h q -> p (h q)")[:, u : 2 * P : 2], ident[:]
            )
        zts[0].append(transpose_words(nc, zt_pool, ident, z_groups[0], UNITS - 1))

        def relaid(h, m):
            first = 32 * h + m
            by_unit = second_turn[HALF * h : HALF * (h + 1), 0 : 2 * P].rearrange("p (u c) -> p u c", u=2)
            return by_unit[:, :, first : first + 3 : 2]

        def second_pass(tile_columns, h):
            return tile_columns[HALF * h : HALF * (h + 1)].rearrange("p (u e) -> p u e", u=2)

        for h in range(2):
            nc.vector.tensor_scalar_add(out=second_pass(var_eps[:, 4:8], h), in0=relaid(h, 1), scalar1=BN_EPS)
        inverse_deviation(1)
        for h in range(2):
            nc.vector.tensor_copy(out=second_pass(mean_var[:, 4:8, 0], h), in_=relaid(h, 0))
        scale_and_shift(1)

        neg_max = const.tile([P, TILES], F32)
        sum_exp = const.tile([P, TILES], F32)
        log_sum = const.tile([P, TILES], F32)
        planes_of, operand_of = {}, {}

        def normalise(c):
            planes = work.tile([P, PASSES, 4, GROUP_ROWS], BF16)
            for unit in range(UNITS):
                for e in range(2):
                    col = 2 * unit + e
                    nc.scalar.activation(
                        out=planes[:, col // 4, col % 4, :],
                        in_=as_pairs(zts[c][unit])[:, :, e],
                        func=ACT.Relu,
                        bias=shift[:, col : col + 1],
                        scale=scale[:, col : col + 1],
                    )
            planes_of[c] = planes

        def regroup(c):
            grouped = work.tile([P, PASSES, GROUP_ROWS, 4], BF16, align_bytes=64)
            for g in range(PASSES):
                nc.vector.tensor_copy(
                    out=grouped[:, g].rearrange("p (c i) t -> p c t i", i=8),
                    in_=planes_of[c][:, g].rearrange("p t (c i) -> p c t i", i=8),
                )
            return grouped

        def quantise(c, grouped):
            codes = work.tile([P, PASSES, GROUP_ROWS], U32, align_bytes=64)
            h_scales = work.tile([P, PASSES, GROUP_ROWS], U8, align_bytes=64)
            nc.vector.quantize_mx(
                out=codes[:].rearrange("p g r -> p (g r)").bitcast(FP8X4),
                scales=h_scales[:].rearrange("p g r -> p (g r)"),
                in_=grouped[:].rearrange("p g r t -> p (g r t)"),
            )
            operand_of[c] = (codes, h_scales)

        def classify(c, pool, tag):
            codes, h_scales = operand_of[c]
            accs = []
            for j in range(GROUP_TILES):
                acc = pool.tile([P, CLASSES], F32, name=tag)
                for g in range(PASSES):
                    nc.tensor.matmul_mx(
                        out=acc[:],
                        lhsT=codes[:, g, P * j : P * (j + 1)].bitcast(FP8X4),
                        lhsT_scale=h_scales[:, g, P * j : P * (j + 1)],
                        rhs=w_words[:, g, :].bitcast(FP4X4),
                        rhs_scale=w_scales[:, g, :],
                        start=(g == 0),
                        stop=(g == PASSES - 1),
                    )
                accs.append(acc)
            return accs

        def logits_and_max(c, accs):
            for j in range(GROUP_TILES + 1):
                if j < GROUP_TILES:
                    nc.vector.tensor_tensor(out=z_groups[c][:, j, :], in0=accs[j][:], in1=bias[:], op=ALU.add)
                if j >= 1:
                    col = GROUP_TILES * c + j - 1
                    nc.vector.tensor_reduce(
                        out=neg_max[:, col : col + 1],
                        in_=z_groups[c][:, j - 1, :],
                        axis=AXIS.X,
                        op=ALU.max,
                        negate=True,
                    )

        def sum_of_exp(c):
            for j in range(GROUP_TILES):
                col = GROUP_TILES * c + j
                unread = scratch.tile([P, CLASSES], BF16)
                nc.scalar.activation(
                    out=unread[:],
                    in_=z_groups[c][:, j, :],
                    func=ACT.Exp,
                    bias=neg_max[:, col : col + 1],
                    scale=1.0,
                    accum_out=sum_exp[:, col : col + 1],
                )

        def shifts(c_from, c_to, engine):
            lo, hi = GROUP_TILES * c_from, GROUP_TILES * c_to
            nc.scalar.activation(out=log_sum[:, lo:hi], in_=sum_exp[:, lo:hi], func=ACT.Ln)
            neg_shift = work.tile([P, LN_GROUPS * GROUP_TILES], F32)
            engine.tensor_tensor(out=neg_shift[:, 0 : hi - lo], in0=neg_max[:, lo:hi], in1=log_sum[:, lo:hi], op=ALU.subtract)
            return neg_shift

        def subtract_and_store(neg_shift, c_first, c, tiles, engine=None):
            for j in tiles:
                col = GROUP_TILES * (c - c_first) + j
                values, shift_of_rows = z_groups[c][:, j, :], neg_shift[:, col : col + 1]
                if engine is None:
                    nc.scalar.activation(out=values, in_=values, func=ACT.Identity, bias=shift_of_rows, scale=1.0)
                else:
                    engine.tensor_scalar(out=values, in0=values, scalar1=1.0, scalar2=shift_of_rows, op0=ALU.mult, op1=ALU.add)
            first = GROUP_TILES * c + tiles[0]
            nc.sync.dma_start(out=out_rows[:, first : first + len(tiles), :], in_=z_groups[c][:, tiles[0] : tiles[0] + len(tiles), :])

        accs_of, grouped_of = {}, {}
        all_tiles = list(range(GROUP_TILES))
        finished = 0
        for k in range(GROUPS + 2):
            if k == GROUPS:
                quantise(k - 1, grouped_of[k - 1])
                accs_of[k - 1] = classify(k - 1, zt_pool, "zt")
            if k >= 2:
                logits_and_max(k - 2, accs_of[k - 2])
            if k < GROUPS:
                normalise(k)
            if k >= 2:
                sum_of_exp(k - 2)
            if k + 1 < GROUPS:
                zts[k + 1] = [transpose_words(nc, zt_pool, ident, z_groups[k + 1], unit) for unit in range(UNITS)]
            if 1 <= k < GROUPS:
                quantise(k - 1, grouped_of[k - 1])
                accs_of[k - 1] = classify(k - 1, acc_pool, "acc")
            if k < GROUPS:
                grouped_of[k] = regroup(k)
            if k == GROUPS + 1:
                subtract_and_store(late_shift, late_first, LATE_GROUP, all_tiles, nc.vector)
            if k - 1 in LN_AFTER and k - 1 < GROUPS:
                neg_shift = shifts(finished, k - 1, nc.gpsimd)
                for c in range(finished, k - 1):
                    if c == LATE_GROUP:
                        late_shift, late_first = neg_shift, finished
                    else:
                        subtract_and_store(neg_shift, finished, c, all_tiles, nc.gpsimd)
                finished = k - 1
        neg_shift = shifts(finished, GROUPS, nc.vector)
        halves = (all_tiles[: GROUP_TILES // 2], all_tiles[GROUP_TILES // 2 :])
        for c in range(finished, GROUPS):
            for i, tiles in enumerate(halves):
                engine = None if c == finished and i == 1 else nc.vector
                subtract_and_store(neg_shift, finished, c, tiles, engine)
